import numpy as np
import ml_dtypes


def mxq(x, axis, fmt="e4m3"):
    dtype, down = {"e4m3": (ml_dtypes.float8_e4m3fn, 7), "e5m2": (ml_dtypes.float8_e5m2, 14)}[fmt]
    v = np.moveaxis(np.asarray(x, np.float32).astype(ml_dtypes.bfloat16).astype(np.float64), axis, -1)
    blocks = v.reshape(v.shape[:-1] + (-1, 32))
    amax = np.abs(blocks).max(-1, keepdims=True)
    byte = np.maximum(np.where(amax > 0, np.frexp(amax)[1] - 1 + 127, 0) - down, 1)
    scale = np.exp2(byte - 127.0)
    codes = (blocks / scale).astype(np.float32).astype(dtype).astype(np.float64)
    return np.moveaxis((codes * scale).reshape(v.shape), -1, axis)


WIDE = False


def mx_kscale(k):
    if not WIDE:
        return np.ones(k)
    levels = np.array([10, -10, 5, -5, 0])
    a = np.random.permutation(np.resize(levels, k // 512 * 4)).reshape(k // 512, 4)
    idx = np.arange(k)
    return np.exp2(a[idx // 512, idx % 128 // 32])


BF16 = ml_dtypes.bfloat16


def bf(x):
    return np.asarray(x, np.float32).astype(BF16)


def f64(x):
    return np.asarray(x).astype(np.float64)


B, C, H, W = 2, 512, 64, 64
N = H * W
KV = 0.05 * N / np.sqrt(C)


def setup_inputs():
    s, t = mx_kscale(C), mx_kscale(C)
    return {"x": bf(np.random.standard_normal((B, C, H, W)) * s[None, :, None, None]),
            "mask": bf(np.random.random_sample((B, 1, H, W))),
            "W_q": bf(np.random.standard_normal((C, C)) / np.sqrt(C) / s[:, None]),
            "b_q": bf(np.random.standard_normal(C) * 0.3),
            "kv_know": bf(np.random.standard_normal((B, 1, C)) * KV * t),
            "kv_mask": bf(np.random.standard_normal((B, 1, C)) * KV * t),
            "W_out": bf(np.random.standard_normal((C, C)) / KV / t[:, None]),
            "b_out": bf(np.random.standard_normal(C) * 0.2)}


def reference(x, mask, W_q, b_q, kv_know, kv_mask, W_out, b_out):
    x, mask = f64(x), f64(mask)
    b, c, h, w = x.shape
    xf = np.transpose(x, (0, 2, 3, 1)).reshape(b, h * w, c)
    q = (mxq(xf, 2, "e4m3") @ mxq(f64(W_q), 0, "e4m3")) + f64(b_q)
    q = q / np.linalg.norm(q, axis=-1, keepdims=True)
    m = np.transpose(mask, (0, 2, 3, 1)).reshape(b, h * w, 1)
    inv = 1.0 - m
    qu = q * inv
    qm = q * m
    out_know = f64(kv_know) * qu
    out_mask = f64(kv_mask) * qm
    out = out_know * inv + m * (0.3 * out_know + 0.7 * out_mask)
    return (mxq(out, 2, "e4m3") @ mxq(f64(W_out), 0, "e4m3")) + f64(b_out)

@@ -1,0 +1,327 @@
+from contextlib import ExitStack
+
+import concourse.mybir as mybir
+from concourse.masks import make_identity
+
+F32 = mybir.dt.float32
+BF16 = mybir.dt.bfloat16
+U32 = mybir.dt.uint32
+U8 = mybir.dt.uint8
+FP8X4 = mybir.dt.float8_e4m3fn_x4
+ACT = mybir.ActivationFunctionType
+ALU = mybir.AluOpType
+
+P = 128
+PACK = 4
+C = 512
+NPIX = 4096
+IMAGES = 2
+CHUNK = 512
+TILES = CHUNK // P
+CHUNKS_PER_IMAGE = NPIX // CHUNK
+N_CHUNKS = IMAGES * CHUNKS_PER_IMAGE
+XLOAD = 1024
+PE_TILES = 3
+
+FLOPS = 2 * 2 * IMAGES * NPIX * C * C
+
+
+def tile_hydraattention_pb_t_kernel(tc, x, mask, W_q, b_q, kv_know, kv_mask, W_out, b_out, out):
+    nc = tc.nc
+    with ExitStack() as ctx:
+        const = ctx.enter_context(tc.tile_pool(name="const", bufs=1))
+        xpool = ctx.enter_context(tc.tile_pool(name="xpool", bufs=1))
+        psum = ctx.enter_context(tc.psum_pool(name="psum", bufs=2))
+
+        x_raw = []
+        wq_codes = const.tile([P, C], U32, name="wq_codes", align_bytes=64)
+        wq_sc = const.tile([P, C], U8, name="wq_sc", align_bytes=64)
+        wo_codes = const.tile([P, C], U32, name="wo_codes", align_bytes=64)
+        wo_sc = const.tile([P, C], U8, name="wo_sc", align_bytes=64)
+        ident_f = const.tile([P, P], F32, name="ident_f")
+        ident_b = const.tile([P, P], BF16, name="ident_b")
+        bq4 = const.tile([P, PACK], F32, name="bq4")
+        bo_b = const.tile([P, C], F32, name="bo_b")
+        ab0 = const.tile([P, N_CHUNKS * TILES, 2], F32, name="ab0")
+        l_rows = [const.tile([P, PACK, P], BF16, name="l_rows%d" % b) for b in range(IMAGES)]
+        kk_b = [const.tile([P, C], F32, name="kk_b%d" % b) for b in range(IMAGES)]
+        km_b = [const.tile([P, C], F32, name="km_b%d" % b) for b in range(IMAGES)]
+        r_in = [const.tile([P, PE_TILES, P], BF16, name="r_in%d" % k) for k in range(2)]
+
+        with tc.tile_pool(name="setup", bufs=1) as setup:
+            wq_raw = setup.tile([P, PACK, C], BF16, name="wq_raw")
+            nc.sync.dma_start(out=wq_raw[:], in_=W_q.rearrange("(p j) c -> p j c", j=PACK))
+            for b in range(IMAGES):
+                xv = x[b].rearrange("(p j) h w -> p j (h w)", j=PACK)
+                for k in range(NPIX // XLOAD):
+                    xr = xpool.tile([P, PACK, XLOAD], BF16, name="x_raw%d_%d" % (b, k))
+                    nc.sync.dma_start(out=xr[:], in_=xv[:, :, k * XLOAD : (k + 1) * XLOAD])
+                    x_raw.append(xr)
+                    if b == 0 and k == 0:
+                        wo_raw = setup.tile([P, PACK, C], BF16, name="wo_raw")
+                        nc.sync.dma_start(out=wo_raw[:], in_=W_out.rearrange("(p j) o -> p j o", j=PACK))
+
+            bq_raw = setup.tile([P, PACK], BF16, name="bq_raw")
+            nc.scalar.dma_start(out=bq_raw[:], in_=b_q.rearrange("(p j) -> p j", j=PACK))
+            m_raw = setup.tile([P, P], BF16, name="m_raw")
+            nc.vector.memset(m_raw[:], 0.0)
+            nc.scalar.dma_start(
+                out=m_raw[0 : N_CHUNKS * TILES, :],
+                in_=mask.rearrange("b o (g h) w -> (b o g) (h w)", h=2),
+            )
+            l_full = []
+            kv_bc = []
+            for b in range(IMAGES):
+                lf = setup.tile([P, C], BF16, name="l_full%d" % b)
+                nc.vector.memset(lf[:], 0.0)
+                nc.scalar.dma_start(out=lf[0:3, :], in_=kv_know[b, 0, :].partition_broadcast(3))
+                nc.scalar.dma_start(out=lf[3:6, :], in_=kv_mask[b, 0, :].partition_broadcast(3))
+                l_full.append(lf)
+                kb = setup.tile([P, C], BF16, name="kkbc%d" % b)
+                nc.scalar.dma_start(out=kb[:], in_=kv_know[b, 0, :].partition_broadcast(P))
+                mb = setup.tile([P, C], BF16, name="kmbc%d" % b)
+                nc.scalar.dma_start(out=mb[:], in_=kv_mask[b, 0, :].partition_broadcast(P))
+                kv_bc.append((kb, mb))
+            bo_raw = setup.tile([P, C], BF16, name="bo_raw")
+            nc.scalar.dma_start(out=bo_raw[:], in_=b_out.partition_broadcast(P))
+
+            warm = setup.tile([P, 1], F32, name="warm")
+            nc.vector.memset(warm[:], 1.0)
+            nc.scalar.activation(out=warm[:], in_=warm[:], func=ACT.Sqrt)
+            make_identity(nc, ident_f[:])
+            make_identity(nc, ident_b[:])
+            for k in range(2):
+                nc.vector.memset(r_in[k][:], 0.0)
+
+            wq_grp = setup.tile([P, C, PACK], BF16, name="wq_grp", align_bytes=64)
+            nc.vector.tensor_copy(
+                out=wq_grp[:].rearrange("q (j p) k -> q j p k", j=PACK),
+                in_=wq_raw[:].rearrange("q k (p j) -> q j p k", j=PACK),
+            )
+            nc.vector.quantize_mx(
+                out=wq_codes[:].bitcast(FP8X4), scales=wq_sc[:], in_=wq_grp[:].rearrange("q c k -> q (c k)")
+            )
+            wo_grp = setup.tile([P, C, PACK], BF16, name="wo_grp", align_bytes=64)
+            nc.vector.tensor_copy(out=wo_grp[:], in_=wo_raw[:].rearrange("p j o -> p o j"))
+            nc.vector.quantize_mx(
+                out=wo_codes[:].bitcast(FP8X4), scales=wo_sc[:], in_=wo_grp[:].rearrange("p o j -> p (o j)")
+            )
+            nc.vector.tensor_copy(out=bq4[:], in_=bq_raw[:])
+            nc.vector.tensor_copy(out=bo_b[:], in_=bo_raw[:])
+            for b in range(IMAGES):
+                nc.vector.tensor_copy(out=l_rows[b][:], in_=l_full[b][:].rearrange("r (p j) -> r j p", j=PACK))
+                nc.vector.tensor_copy(
+                    out=kk_b[b][:].rearrange("q (j p) -> q j p", j=PACK),
+                    in_=kv_bc[b][0][:].rearrange("q (p j) -> q j p", j=PACK),
+                )
+                nc.vector.tensor_copy(
+                    out=km_b[b][:].rearrange("q (j p) -> q j p", j=PACK),
+                    in_=kv_bc[b][1][:].rearrange("q (p j) -> q j p", j=PACK),
+                )
+
+            m_ps = psum.tile([P, P], BF16, name="m_ps", tag="ut")
+            nc.tensor.transpose(m_ps[:], m_raw[:], ident_b[:])
+            nt = N_CHUNKS * TILES
+            m_t = setup.tile([P, nt], F32, name="m_t")
+            nc.vector.tensor_copy(out=m_t[:], in_=m_ps[:, 0:nt])
+            inv = setup.tile([P, nt], F32, name="inv")
+            nc.vector.tensor_scalar(out=inv[:], in0=m_t[:], scalar1=-1.0, scalar2=1.0, op0=ALU.mult, op1=ALU.add)
+            mix = setup.tile([P, nt], F32, name="mix")
+            nc.vector.scalar_tensor_tensor(out=mix[:], in0=m_t[:], scalar=0.3, in1=inv[:], op0=ALU.mult, op1=ALU.add)
+            nc.vector.tensor_tensor(out=ab0[:, :, 0], in0=inv[:], in1=mix[:], op=ALU.mult)
+            nc.vector.scalar_tensor_tensor(
+                out=ab0[:, :, 1], in0=m_t[:], scalar=0.7, in1=m_t[:], op0=ALU.mult, op1=ALU.mult
+            )
+
+        xq = ctx.enter_context(tc.tile_pool(name="xq", bufs=3))
+        upool = ctx.enter_context(tc.tile_pool(name="upool", bufs=5))
+        small = ctx.enter_context(tc.tile_pool(name="small", bufs=3))
+        work = ctx.enter_context(tc.tile_pool(name="work", bufs=2))
+        gq = ctx.enter_context(tc.tile_pool(name="gq", bufs=3))
+        ypool = ctx.enter_context(tc.tile_pool(name="ypool", bufs=3))
+
+        state = {}
+
+        def live(i):
+            return 0 <= i < N_CHUNKS
+
+        def regroup_x(i):
+            xr = x_raw[i // 2]
+            off = (i % 2) * CHUNK
+            xg = work.tile([P, CHUNK, PACK], BF16, name="xg", align_bytes=64)
+            nc.gpsimd.tensor_scalar(
+                out=xg[:],
+                in0=xr[:, :, off : off + CHUNK].rearrange("p j t -> p t j"),
+                scalar1=1.0,
+                scalar2=0.0,
+                op0=ALU.mult,
+                op1=ALU.add,
+            )
+            state[("xg", i)] = xg
+
+        def quantise_x(i):
+            xg = state[("xg", i)]
+            xc = xq.tile([P, CHUNK], U32, name="xc", align_bytes=64)
+            xs = xq.tile([P, CHUNK], U8, name="xs", align_bytes=64)
+            nc.vector.quantize_mx(out=xc[:].bitcast(FP8X4), scales=xs[:], in_=xg[:].rearrange("p t j -> p (t j)"))
+            state[("x", i)] = (xc, xs)
+
+        def project_q(i, j):
+            xc, xs = state[("x", i)]
+            if j == 0:
+                state[("u", i)] = upool.tile([P, PACK, CHUNK], F32, name="u")
+            u = state[("u", i)]
+            q = psum.tile([P, CHUNK], F32, name="q", tag="q")
+            nc.tensor.matmul_mx(
+                out=q[:],
+                lhsT=wq_codes[:, j * P : (j + 1) * P].bitcast(FP8X4),
+                lhsT_scale=wq_sc[:, j * P : (j + 1) * P],
+                rhs=xc[:].bitcast(FP8X4),
+                rhs_scale=xs[:],
+                start=True,
+                stop=True,
+            )
+            nc.scalar.activation(out=u[:, j, :], in_=q[:], func=ACT.Identity, bias=bq4[:, j : j + 1], scale=1.0)
+
+        def square_sum(i, tt):
+            u = state[("u", i)]
+            if tt == 0:
+                state[("n2", i)] = small.tile([P, TILES], F32, name="n2")
+            n2 = state[("n2", i)]
+            ut = psum.tile([P, C], F32, name="ut", tag="ut")
+            for j in range(PACK):
+                nc.tensor.transpose(ut[:, j * P : (j + 1) * P], u[:, j, tt * P : (tt + 1) * P], ident_f[:])
+            junk = work.tile([P, C], BF16, name="junk")
+            nc.scalar.activation(out=junk[:], in_=ut[:], func=ACT.Square, accum_out=n2[:, tt : tt + 1])
+
+        def norm(i):
+            nrm = small.tile([P, TILES], F32, name="nrm")
+            nc.scalar.activation(out=nrm[:], in_=state[("n2", i)][:], func=ACT.Sqrt)
+            state[("nrm", i)] = nrm
+
+        def factors(i):
+            rn = small.tile([P, TILES], F32, name="rn")
+            nc.vector.reciprocal(out=rn[:], in_=state[("nrm", i)][:])
+            ab = small.tile([P, TILES, 2], F32, name="ab")
+            nc.vector.tensor_tensor(
+                out=ab[:],
+                in0=ab0[:, i * TILES : (i + 1) * TILES, :],
+                in1=rn[:].unsqueeze(2).to_broadcast([P, TILES, 2]),
+                op=ALU.mult,
+            )
+            state[("ab", i)] = ab
+
+        def pieces(i):
+            ab = state[("ab", i)]
+            rin = r_in[i % 2]
+            nc.gpsimd.tensor_copy(out=rin[:, :, 0:6:3], in_=ab[:, 0:PE_TILES, :])
+            r1 = small.tile([P, PE_TILES, 2], F32, name="r1")
+            nc.gpsimd.tensor_tensor(out=r1[:], in0=ab[:, 0:PE_TILES, :], in1=rin[:, :, 0:6:3], op=ALU.subtract)
+            nc.gpsimd.tensor_copy(out=rin[:, :, 1:6:3], in_=r1[:])
+            r2 = small.tile([P, PE_TILES, 2], F32, name="r2")
+            nc.gpsimd.tensor_tensor(out=r2[:], in0=r1[:], in1=rin[:, :, 1:6:3], op=ALU.subtract)
+            nc.gpsimd.tensor_copy(out=rin[:, :, 2:6:3], in_=r2[:])
+
+        def gate_last_tile(i):
+            b = i // CHUNKS_PER_IMAGE
+            ab = state[("ab", i)]
+            zk = work.tile([P, C], F32, name="zk")
+            nc.scalar.activation(out=zk[:], in_=kk_b[b][:], func=ACT.Copy, scale=ab[:, PE_TILES, 0:1])
+            zm = work.tile([P, C], F32, name="zm")
+            nc.scalar.activation(out=zm[:], in_=km_b[b][:], func=ACT.Copy, scale=ab[:, PE_TILES, 1:2])
+            wt = work.tile([P, C], F32, name="wt")
+            nc.gpsimd.tensor_tensor(out=wt[:], in0=zk[:], in1=zm[:], op=ALU.add)
+            state[("wt", i)] = wt
+
+        def factor_rows(i):
+            rin = r_in[i % 2]
+            rp = psum.tile([P, PE_TILES, P], BF16, name="rp", tag="ut")
+            for tt in range(PE_TILES):
+                nc.tensor.transpose(rp[:, tt, :], rin[:, tt, :], ident_b[:])
+            rows = work.tile([P, PE_TILES, P], BF16, name="rows")
+            nc.scalar.copy(out=rows[:], in_=rp[:])
+            state[("rows", i)] = rows
+
+        def gate(i, tt):
+            b = i // CHUNKS_PER_IMAGE
+            u = state[("u", i)]
+            if tt == 0:
+                state[("gg", i)] = work.tile([P, CHUNK, PACK], BF16, name="gg", align_bytes=64)
+            gg = state[("gg", i)]
+            wb = psum.tile([P, PACK, P], F32, name="wb", tag="wb")
+            if tt < PE_TILES:
+                rows = state[("rows", i)]
+                for j in range(PACK):
+                    nc.tensor.matmul(out=wb[:, j, :], lhsT=l_rows[b][:, j, :], rhs=rows[:, tt, :], start=True, stop=True)
+            else:
+                wt = state[("wt", i)]
+                for j in range(PACK):
+                    nc.tensor.transpose(wb[:, j, :], wt[:, j * P : (j + 1) * P], ident_f[:])
+            nc.vector.tensor_tensor(
+                out=gg[:, tt * P : (tt + 1) * P, :],
+                in0=u[:, :, tt * P : (tt + 1) * P].rearrange("p j t -> p t j"),
+                in1=wb[:].rearrange("p j t -> p t j"),
+                op=ALU.mult,
+            )
+
+        def quantise_g(i):
+            gg = state[("gg", i)]
+            gc = gq.tile([P, CHUNK], U32, name="gc", align_bytes=64)
+            gs = gq.tile([P, CHUNK], U8, name="gs", align_bytes=64)
+            nc.vector.quantize_mx(out=gc[:].bitcast(FP8X4), scales=gs[:], in_=gg[:].rearrange("p t j -> p (t j)"))
+            state[("g", i)] = (gc, gs)
+
+        def project_out(i, tt):
+            gc, gs = state[("g", i)]
+            if tt == 0:
+                state[("yo", i)] = ypool.tile([P, TILES, C], F32, name="yo")
+            yo = state[("yo", i)]
+            y = psum.tile([P, C], F32, name="y", tag="y")
+            nc.tensor.matmul_mx(
+                out=y[:],
+                lhsT=gc[:, tt * P : (tt + 1) * P].bitcast(FP8X4),
+                lhsT_scale=gs[:, tt * P : (tt + 1) * P],
+                rhs=wo_codes[:].bitcast(FP8X4),
+                rhs_scale=wo_sc[:],
+                start=True,
+                stop=True,
+            )
+            nc.vector.tensor_tensor(out=yo[:, tt, :], in0=y[:], in1=bo_b[:], op=ALU.add)
+
+        def store(i):
+            b = i // CHUNKS_PER_IMAGE
+            t0 = (i % CHUNKS_PER_IMAGE) * CHUNK
+            nc.sync.dma_start(
+                out=out[b, t0 : t0 + CHUNK, :].rearrange("(tt p) o -> p tt o", p=P), in_=state[("yo", i)][:]
+            )
+
+        with tc.manual_schedule():
+            for s in range(N_CHUNKS + 6):
+                if live(s - 4):
+                    pieces(s - 4)
+                for k in range(TILES):
+                    if live(s - 6):
+                        project_out(s - 6, k)
+                    if live(s - 2):
+                        project_q(s - 2, k)
+                if live(s - 6):
+                    store(s - 6)
+                if live(s):
+                    regroup_x(s)
+                if live(s - 4):
+                    factor_rows(s - 4)
+                for k in range(TILES):
+                    if live(s - 3):
+                        square_sum(s - 3, k)
+                    if live(s - 5):
+                        gate(s - 5, k)
+                if live(s - 3):
+                    norm(s - 3)
+                if live(s - 5):
+                    quantise_g(s - 5)
+                if live(s - 1):
+                    quantise_x(s - 1)
+                if live(s - 3):
+                    factors(s - 3)
+                if live(s - 4):
+                    gate_last_tile(s - 4)

@@ -20,6 +20,7 @@ CHUNK = 512
 TILES = CHUNK // P
 CHUNKS_PER_IMAGE = NPIX // CHUNK
 N_CHUNKS = IMAGES * CHUNKS_PER_IMAGE
+N_TILES = N_CHUNKS * TILES
 XLOAD = 1024
 PE_TILES = 3
 
@@ -31,9 +32,14 @@ def tile_hydraattention_pb_t_kernel(tc, x, mask, W_q, b_q, kv_know, kv_mask, W_o
     with ExitStack() as ctx:
         const = ctx.enter_context(tc.tile_pool(name="const", bufs=1))
         xpool = ctx.enter_context(tc.tile_pool(name="xpool", bufs=1))
-        psum = ctx.enter_context(tc.psum_pool(name="psum", bufs=2))
+        psum = ctx.enter_context(tc.psum_pool(name="psum", bufs=4))
+        xq = ctx.enter_context(tc.tile_pool(name="xq", bufs=3))
+        upool = ctx.enter_context(tc.tile_pool(name="upool", bufs=5))
+        small = ctx.enter_context(tc.tile_pool(name="small", bufs=3))
+        work = ctx.enter_context(tc.tile_pool(name="work", bufs=2))
+        gq = ctx.enter_context(tc.tile_pool(name="gq", bufs=3))
+        ypool = ctx.enter_context(tc.tile_pool(name="ypool", bufs=3))
 
-        x_raw = []
         wq_codes = const.tile([P, C], U32, name="wq_codes", align_bytes=64)
         wq_sc = const.tile([P, C], U8, name="wq_sc", align_bytes=64)
         wo_codes = const.tile([P, C], U32, name="wo_codes", align_bytes=64)
@@ -42,72 +48,84 @@ def tile_hydraattention_pb_t_kernel(tc, x, mask, W_q, b_q, kv_know, kv_mask, W_o
         ident_b = const.tile([P, P], BF16, name="ident_b")
         bq4 = const.tile([P, PACK], F32, name="bq4")
         bo_b = const.tile([P, C], F32, name="bo_b")
-        ab0 = const.tile([P, N_CHUNKS * TILES, 2], F32, name="ab0")
+        ab0 = const.tile([P, N_TILES, 2], F32, name="ab0")
         l_rows = [const.tile([P, PACK, P], BF16, name="l_rows%d" % b) for b in range(IMAGES)]
         kk_b = [const.tile([P, C], F32, name="kk_b%d" % b) for b in range(IMAGES)]
         km_b = [const.tile([P, C], F32, name="km_b%d" % b) for b in range(IMAGES)]
         r_in = [const.tile([P, PE_TILES, P], BF16, name="r_in%d" % k) for k in range(2)]
 
-        with tc.tile_pool(name="setup", bufs=1) as setup:
-            wq_raw = setup.tile([P, PACK, C], BF16, name="wq_raw")
-            nc.sync.dma_start(out=wq_raw[:], in_=W_q.rearrange("(p j) c -> p j c", j=PACK))
-            for b in range(IMAGES):
-                xv = x[b].rearrange("(p j) h w -> p j (h w)", j=PACK)
-                for k in range(NPIX // XLOAD):
-                    xr = xpool.tile([P, PACK, XLOAD], BF16, name="x_raw%d_%d" % (b, k))
+        wq_raw = work.tile([P, PACK, C], BF16, name="wq_raw", tag="gg", align_bytes=64)
+        nc.sync.dma_start(out=wq_raw[:], in_=W_q.rearrange("(p j) c -> p j c", j=PACK))
+        wo_raw = work.tile([P, PACK, C], BF16, name="wo_raw", tag="gg", align_bytes=64)
+        x_raw = []
+        for b in range(IMAGES):
+            xv = x[b].rearrange("(p j) h w -> p j (h w)", j=PACK)
+            for k in range(NPIX // XLOAD):
+                xr = xpool.tile([P, PACK, XLOAD], BF16, name="x_raw%d_%d" % (b, k))
+                if b == 0 and k == 0:
+                    nc.sync.dma_start(out=xr[:, :, 0:CHUNK], in_=xv[:, :, 0:CHUNK])
+                    nc.sync.dma_start(out=xr[:, :, CHUNK:XLOAD], in_=xv[:, :, CHUNK:XLOAD])
+                else:
                     nc.sync.dma_start(out=xr[:], in_=xv[:, :, k * XLOAD : (k + 1) * XLOAD])
-                    x_raw.append(xr)
-                    if b == 0 and k == 0:
-                        wo_raw = setup.tile([P, PACK, C], BF16, name="wo_raw")
-                        nc.sync.dma_start(out=wo_raw[:], in_=W_out.rearrange("(p j) o -> p j o", j=PACK))
+                x_raw.append(xr)
+                if b == 0 and k == 1:
+                    nc.sync.dma_start(out=wo_raw[:], in_=W_out.rearrange("(p j) o -> p j o", j=PACK))
 
-            bq_raw = setup.tile([P, PACK], BF16, name="bq_raw")
-            nc.scalar.dma_start(out=bq_raw[:], in_=b_q.rearrange("(p j) -> p j", j=PACK))
-            m_raw = setup.tile([P, P], BF16, name="m_raw")
-            nc.vector.memset(m_raw[:], 0.0)
-            nc.scalar.dma_start(
-                out=m_raw[0 : N_CHUNKS * TILES, :],
-                in_=mask.rearrange("b o (g h) w -> (b o g) (h w)", h=2),
-            )
-            l_full = []
-            kv_bc = []
-            for b in range(IMAGES):
-                lf = setup.tile([P, C], BF16, name="l_full%d" % b)
-                nc.vector.memset(lf[:], 0.0)
-                nc.scalar.dma_start(out=lf[0:3, :], in_=kv_know[b, 0, :].partition_broadcast(3))
-                nc.scalar.dma_start(out=lf[3:6, :], in_=kv_mask[b, 0, :].partition_broadcast(3))
-                l_full.append(lf)
-                kb = setup.tile([P, C], BF16, name="kkbc%d" % b)
-                nc.scalar.dma_start(out=kb[:], in_=kv_know[b, 0, :].partition_broadcast(P))
-                mb = setup.tile([P, C], BF16, name="kmbc%d" % b)
-                nc.scalar.dma_start(out=mb[:], in_=kv_mask[b, 0, :].partition_broadcast(P))
-                kv_bc.append((kb, mb))
-            bo_raw = setup.tile([P, C], BF16, name="bo_raw")
-            nc.scalar.dma_start(out=bo_raw[:], in_=b_out.partition_broadcast(P))
+        bq_raw = const.tile([P, PACK], BF16, name="bq_raw")
+        nc.scalar.dma_start(out=bq_raw[:], in_=b_q.rearrange("(p j) -> p j", j=PACK))
+        m_raw = const.tile([P, P], BF16, name="m_raw")
+        nc.vector.memset(m_raw[:], 0.0)
+        nc.scalar.dma_start(out=m_raw[0:N_TILES, :], in_=mask.rearrange("b o (g h) w -> (b o g) (h w)", h=2))
+        l_full = []
+        kv_bc = []
+        for b in range(IMAGES):
+            lf = const.tile([P, C], BF16, name="l_full%d" % b)
+            nc.vector.memset(lf[:], 0.0)
+            nc.scalar.dma_start(out=lf[0:3, :], in_=kv_know[b, 0, :].partition_broadcast(3))
+            nc.scalar.dma_start(out=lf[3:6, :], in_=kv_mask[b, 0, :].partition_broadcast(3))
+            l_full.append(lf)
+        for b in range(IMAGES):
+            kb = const.tile([P, C], BF16, name="kkbc%d" % b)
+            nc.scalar.dma_start(out=kb[:], in_=kv_know[b, 0, :].partition_broadcast(P))
+            mb = const.tile([P, C], BF16, name="kmbc%d" % b)
+            nc.scalar.dma_start(out=mb[:], in_=kv_mask[b, 0, :].partition_broadcast(P))
+            kv_bc.append((kb, mb))
+        bo_raw = const.tile([P, C], BF16, name="bo_raw")
+        nc.scalar.dma_start(out=bo_raw[:], in_=b_out.partition_broadcast(P))
 
-            warm = setup.tile([P, 1], F32, name="warm")
-            nc.vector.memset(warm[:], 1.0)
-            nc.scalar.activation(out=warm[:], in_=warm[:], func=ACT.Sqrt)
-            make_identity(nc, ident_f[:])
-            make_identity(nc, ident_b[:])
-            for k in range(2):
-                nc.vector.memset(r_in[k][:], 0.0)
+        warm = const.tile([P, 1], F32, name="warm")
+        nc.vector.memset(warm[:], 1.0)
+        nc.scalar.activation(out=warm[:], in_=warm[:], func=ACT.Sqrt)
+        make_identity(nc, ident_b[:])
+        make_identity(nc, ident_f[:])
+        for k in range(2):
+            nc.vector.memset(r_in[k][:], 0.0)
 
-            wq_grp = setup.tile([P, C, PACK], BF16, name="wq_grp", align_bytes=64)
-            nc.vector.tensor_copy(
-                out=wq_grp[:].rearrange("q (j p) k -> q j p k", j=PACK),
-                in_=wq_raw[:].rearrange("q k (p j) -> q j p k", j=PACK),
+        wq_grp = work.tile([P, C, PACK], BF16, name="wq_grp", tag="xg", align_bytes=64)
+        nc.vector.tensor_copy(
+            out=wq_grp[:].rearrange("q (j p) k -> q j p k", j=PACK),
+            in_=wq_raw[:].rearrange("q k (p j) -> q j p k", j=PACK),
+        )
+        nc.vector.quantize_mx(
+            out=wq_codes[:].bitcast(FP8X4), scales=wq_sc[:], in_=wq_grp[:].rearrange("q c k -> q (c k)")
+        )
+        nc.vector.tensor_copy(out=bq4[:], in_=bq_raw[:])
+
+        def setup_mask():
+            m_ps = psum.tile([P, P], BF16, name="m_ps", tag="sd")
+            nc.tensor.transpose(m_ps[:], m_raw[:], ident_b[:])
+            m_t = const.tile([P, N_TILES], F32, name="m_t")
+            nc.vector.tensor_copy(out=m_t[:], in_=m_ps[:, 0:N_TILES])
+            inv = const.tile([P, N_TILES], F32, name="inv")
+            nc.vector.tensor_scalar(out=inv[:], in0=m_t[:], scalar1=-1.0, scalar2=1.0, op0=ALU.mult, op1=ALU.add)
+            mix = const.tile([P, N_TILES], F32, name="mix")
+            nc.vector.scalar_tensor_tensor(out=mix[:], in0=m_t[:], scalar=0.3, in1=inv[:], op0=ALU.mult, op1=ALU.add)
+            nc.vector.tensor_tensor(out=ab0[:, :, 0], in0=inv[:], in1=mix[:], op=ALU.mult)
+            nc.vector.scalar_tensor_tensor(
+                out=ab0[:, :, 1], in0=m_t[:], scalar=0.7, in1=m_t[:], op0=ALU.mult, op1=ALU.mult
             )
-            nc.vector.quantize_mx(
-                out=wq_codes[:].bitcast(FP8X4), scales=wq_sc[:], in_=wq_grp[:].rearrange("q c k -> q (c k)")
-            )
-            wo_grp = setup.tile([P, C, PACK], BF16, name="wo_grp", align_bytes=64)
-            nc.vector.tensor_copy(out=wo_grp[:], in_=wo_raw[:].rearrange("p j o -> p o j"))
-            nc.vector.quantize_mx(
-                out=wo_codes[:].bitcast(FP8X4), scales=wo_sc[:], in_=wo_grp[:].rearrange("p o j -> p (o j)")
-            )
-            nc.vector.tensor_copy(out=bq4[:], in_=bq_raw[:])
-            nc.vector.tensor_copy(out=bo_b[:], in_=bo_raw[:])
+
+        def setup_kv():
             for b in range(IMAGES):
                 nc.vector.tensor_copy(out=l_rows[b][:], in_=l_full[b][:].rearrange("r (p j) -> r j p", j=PACK))
                 nc.vector.tensor_copy(
@@ -119,26 +137,13 @@ def tile_hydraattention_pb_t_kernel(tc, x, mask, W_q, b_q, kv_know, kv_mask, W_o
                     in_=kv_bc[b][1][:].rearrange("q (p j) -> q j p", j=PACK),
                 )
 
-            m_ps = psum.tile([P, P], BF16, name="m_ps", tag="ut")
-            nc.tensor.transpose(m_ps[:], m_raw[:], ident_b[:])
-            nt = N_CHUNKS * TILES
-            m_t = setup.tile([P, nt], F32, name="m_t")
-            nc.vector.tensor_copy(out=m_t[:], in_=m_ps[:, 0:nt])
-            inv = setup.tile([P, nt], F32, name="inv")
-            nc.vector.tensor_scalar(out=inv[:], in0=m_t[:], scalar1=-1.0, scalar2=1.0, op0=ALU.mult, op1=ALU.add)
-            mix = setup.tile([P, nt], F32, name="mix")
-            nc.vector.scalar_tensor_tensor(out=mix[:], in0=m_t[:], scalar=0.3, in1=inv[:], op0=ALU.mult, op1=ALU.add)
-            nc.vector.tensor_tensor(out=ab0[:, :, 0], in0=inv[:], in1=mix[:], op=ALU.mult)
-            nc.vector.scalar_tensor_tensor(
-                out=ab0[:, :, 1], in0=m_t[:], scalar=0.7, in1=m_t[:], op0=ALU.mult, op1=ALU.mult
+        def setup_out():
+            wo_grp = work.tile([P, C, PACK], BF16, name="wo_grp", tag="gg", align_bytes=64)
+            nc.vector.tensor_copy(out=wo_grp[:], in_=wo_raw[:].rearrange("p j o -> p o j"))
+            nc.vector.tensor_copy(out=bo_b[:], in_=bo_raw[:])
+            nc.vector.quantize_mx(
+                out=wo_codes[:].bitcast(FP8X4), scales=wo_sc[:], in_=wo_grp[:].rearrange("p o j -> p (o j)")
             )
-
-        xq = ctx.enter_context(tc.tile_pool(name="xq", bufs=3))
-        upool = ctx.enter_context(tc.tile_pool(name="upool", bufs=5))
-        small = ctx.enter_context(tc.tile_pool(name="small", bufs=3))
-        work = ctx.enter_context(tc.tile_pool(name="work", bufs=2))
-        gq = ctx.enter_context(tc.tile_pool(name="gq", bufs=3))
-        ypool = ctx.enter_context(tc.tile_pool(name="ypool", bufs=3))
 
         state = {}
 
@@ -171,7 +176,7 @@ def tile_hydraattention_pb_t_kernel(tc, x, mask, W_q, b_q, kv_know, kv_mask, W_o
             if j == 0:
                 state[("u", i)] = upool.tile([P, PACK, CHUNK], F32, name="u")
             u = state[("u", i)]
-            q = psum.tile([P, CHUNK], F32, name="q", tag="q")
+            q = psum.tile([P, CHUNK], F32, name="q", tag="sd")
             nc.tensor.matmul_mx(
                 out=q[:],
                 lhsT=wq_codes[:, j * P : (j + 1) * P].bitcast(FP8X4),
@@ -188,7 +193,7 @@ def tile_hydraattention_pb_t_kernel(tc, x, mask, W_q, b_q, kv_know, kv_mask, W_o
             if tt == 0:
                 state[("n2", i)] = small.tile([P, TILES], F32, name="n2")
             n2 = state[("n2", i)]
-            ut = psum.tile([P, C], F32, name="ut", tag="ut")
+            ut = psum.tile([P, C], F32, name="ut", tag="sd")
             for j in range(PACK):
                 nc.tensor.transpose(ut[:, j * P : (j + 1) * P], u[:, j, tt * P : (tt + 1) * P], ident_f[:])
             junk = work.tile([P, C], BF16, name="junk")
@@ -235,7 +240,7 @@ def tile_hydraattention_pb_t_kernel(tc, x, mask, W_q, b_q, kv_know, kv_mask, W_o
 
         def factor_rows(i):
             rin = r_in[i % 2]
-            rp = psum.tile([P, PE_TILES, P], BF16, name="rp", tag="ut")
+            rp = psum.tile([P, PE_TILES, P], BF16, name="rp", tag="sd")
             for tt in range(PE_TILES):
                 nc.tensor.transpose(rp[:, tt, :], rin[:, tt, :], ident_b[:])
             rows = work.tile([P, PE_TILES, P], BF16, name="rows")
@@ -248,7 +253,7 @@ def tile_hydraattention_pb_t_kernel(tc, x, mask, W_q, b_q, kv_know, kv_mask, W_o
             if tt == 0:
                 state[("gg", i)] = work.tile([P, CHUNK, PACK], BF16, name="gg", align_bytes=64)
             gg = state[("gg", i)]
-            wb = psum.tile([P, PACK, P], F32, name="wb", tag="wb")
+            wb = psum.tile([P, PACK, P], F32, name="wb", tag="vd")
             if tt < PE_TILES:
                 rows = state[("rows", i)]
                 for j in range(PACK):
@@ -276,7 +281,7 @@ def tile_hydraattention_pb_t_kernel(tc, x, mask, W_q, b_q, kv_know, kv_mask, W_o
             if tt == 0:
                 state[("yo", i)] = ypool.tile([P, TILES, C], F32, name="yo")
             yo = state[("yo", i)]
-            y = psum.tile([P, C], F32, name="y", tag="y")
+            y = psum.tile([P, C], F32, name="y", tag="vd")
             nc.tensor.matmul_mx(
                 out=y[:],
                 lhsT=gc[:, tt * P : (tt + 1) * P].bitcast(FP8X4),
@@ -296,20 +301,20 @@ def tile_hydraattention_pb_t_kernel(tc, x, mask, W_q, b_q, kv_know, kv_mask, W_o
             )
 
         with tc.manual_schedule():
-            for s in range(N_CHUNKS + 6):
+            for s in range(N_CHUNKS + 7):
                 if live(s - 4):
                     pieces(s - 4)
-                for k in range(TILES):
-                    if live(s - 6):
-                        project_out(s - 6, k)
-                    if live(s - 2):
-                        project_q(s - 2, k)
-                if live(s - 6):
-                    store(s - 6)
                 if live(s):
                     regroup_x(s)
-                if live(s - 4):
-                    factor_rows(s - 4)
+                for k in range(TILES):
+                    if live(s - 7):
+                        project_out(s - 7, k)
+                    if live(s - 2):
+                        project_q(s - 2, k)
+                if live(s - 7):
+                    store(s - 7)
+                if live(s - 1):
+                    quantise_x(s - 1)
                 for k in range(TILES):
                     if live(s - 3):
                         square_sum(s - 3, k)
@@ -319,9 +324,14 @@ def tile_hydraattention_pb_t_kernel(tc, x, mask, W_q, b_q, kv_know, kv_mask, W_o
                     norm(s - 3)
                 if live(s - 5):
                     quantise_g(s - 5)
-                if live(s - 1):
-                    quantise_x(s - 1)
+                if s == 1:
+                    setup_mask()
+                if s == 2:
+                    setup_kv()
+                if s == 3:
+                    setup_out()
                 if live(s - 3):
                     factors(s - 3)
                 if live(s - 4):
                     gate_last_tile(s - 4)
+                    factor_rows(s - 4)

@@ -38,6 +38,7 @@ def tile_hydraattention_pb_t_kernel(tc, x, mask, W_q, b_q, kv_know, kv_mask, W_o
         small = ctx.enter_context(tc.tile_pool(name="small", bufs=3))
         work = ctx.enter_context(tc.tile_pool(name="work", bufs=2))
         gq = ctx.enter_context(tc.tile_pool(name="gq", bufs=3))
+        xgp = ctx.enter_context(tc.tile_pool(name="xgp", bufs=1))
         ypool = ctx.enter_context(tc.tile_pool(name="ypool", bufs=3))
 
         wq_codes = const.tile([P, C], U32, name="wq_codes", align_bytes=64)
@@ -101,7 +102,7 @@ def tile_hydraattention_pb_t_kernel(tc, x, mask, W_q, b_q, kv_know, kv_mask, W_o
         for k in range(2):
             nc.vector.memset(r_in[k][:], 0.0)
 
-        wq_grp = work.tile([P, C, PACK], BF16, name="wq_grp", tag="xg", align_bytes=64)
+        wq_grp = xgp.tile([P, C, PACK], BF16, name="wq_grp", tag="xg", align_bytes=64)
         nc.vector.tensor_copy(
             out=wq_grp[:].rearrange("q (j p) k -> q j p k", j=PACK),
             in_=wq_raw[:].rearrange("q k (p j) -> q j p k", j=PACK),
@@ -153,7 +154,7 @@ def tile_hydraattention_pb_t_kernel(tc, x, mask, W_q, b_q, kv_know, kv_mask, W_o
         def regroup_x(i):
             xr = x_raw[i // 2]
             off = (i % 2) * CHUNK
-            xg = work.tile([P, CHUNK, PACK], BF16, name="xg", align_bytes=64)
+            xg = xgp.tile([P, CHUNK, PACK], BF16, name="xg", tag="xg", align_bytes=64)
             nc.gpsimd.tensor_scalar(
                 out=xg[:],
                 in0=xr[:, :, off : off + CHUNK].rearrange("p j t -> p t j"),
@@ -204,28 +205,29 @@ def tile_hydraattention_pb_t_kernel(tc, x, mask, W_q, b_q, kv_know, kv_mask, W_o
             nc.scalar.activation(out=nrm[:], in_=state[("n2", i)][:], func=ACT.Sqrt)
             state[("nrm", i)] = nrm
 
-        def factors(i):
+        def factor_chain(i):
+            nrm = state[("nrm", i)]
             rn = small.tile([P, TILES], F32, name="rn")
-            nc.vector.reciprocal(out=rn[:], in_=state[("nrm", i)][:])
             ab = small.tile([P, TILES, 2], F32, name="ab")
-            nc.vector.tensor_tensor(
-                out=ab[:],
-                in0=ab0[:, i * TILES : (i + 1) * TILES, :],
-                in1=rn[:].unsqueeze(2).to_broadcast([P, TILES, 2]),
-                op=ALU.mult,
-            )
-            state[("ab", i)] = ab
-
-        def pieces(i):
-            ab = state[("ab", i)]
-            rin = r_in[i % 2]
-            nc.gpsimd.tensor_copy(out=rin[:, :, 0:6:3], in_=ab[:, 0:PE_TILES, :])
             r1 = small.tile([P, PE_TILES, 2], F32, name="r1")
-            nc.gpsimd.tensor_tensor(out=r1[:], in0=ab[:, 0:PE_TILES, :], in1=rin[:, :, 0:6:3], op=ALU.subtract)
-            nc.gpsimd.tensor_copy(out=rin[:, :, 1:6:3], in_=r1[:])
             r2 = small.tile([P, PE_TILES, 2], F32, name="r2")
-            nc.gpsimd.tensor_tensor(out=r2[:], in0=r1[:], in1=rin[:, :, 1:6:3], op=ALU.subtract)
-            nc.gpsimd.tensor_copy(out=rin[:, :, 2:6:3], in_=r2[:])
+            rin = r_in[i % 2]
+            head = ab[:, 0:PE_TILES, :]
+            state[("ab", i)] = ab
+            return [
+                lambda: nc.vector.reciprocal(out=rn[:], in_=nrm[:]),
+                lambda: nc.vector.tensor_tensor(
+                    out=ab[:],
+                    in0=ab0[:, i * TILES : (i + 1) * TILES, :],
+                    in1=rn[:].unsqueeze(2).to_broadcast([P, TILES, 2]),
+                    op=ALU.mult,
+                ),
+                lambda: nc.vector.tensor_copy(out=rin[:, :, 0:6:3], in_=head),
+                lambda: nc.vector.tensor_tensor(out=r1[:], in0=head, in1=rin[:, :, 0:6:3], op=ALU.subtract),
+                lambda: nc.vector.tensor_copy(out=rin[:, :, 1:6:3], in_=r1[:]),
+                lambda: nc.vector.tensor_tensor(out=r2[:], in0=r1[:], in1=rin[:, :, 1:6:3], op=ALU.subtract),
+                lambda: nc.vector.tensor_copy(out=rin[:, :, 2:6:3], in_=r2[:]),
+            ]
 
         def gate_last_tile(i):
             b = i // CHUNKS_PER_IMAGE
@@ -234,9 +236,7 @@ def tile_hydraattention_pb_t_kernel(tc, x, mask, W_q, b_q, kv_know, kv_mask, W_o
             nc.scalar.activation(out=zk[:], in_=kk_b[b][:], func=ACT.Copy, scale=ab[:, PE_TILES, 0:1])
             zm = work.tile([P, C], F32, name="zm")
             nc.scalar.activation(out=zm[:], in_=km_b[b][:], func=ACT.Copy, scale=ab[:, PE_TILES, 1:2])
-            wt = work.tile([P, C], F32, name="wt")
-            nc.gpsimd.tensor_tensor(out=wt[:], in0=zk[:], in1=zm[:], op=ALU.add)
-            state[("wt", i)] = wt
+            state[("wt", i)] = (zk, zm)
 
         def factor_rows(i):
             rin = r_in[i % 2]
@@ -259,9 +259,15 @@ def tile_hydraattention_pb_t_kernel(tc, x, mask, W_q, b_q, kv_know, kv_mask, W_o
                 for j in range(PACK):
                     nc.tensor.matmul(out=wb[:, j, :], lhsT=l_rows[b][:, j, :], rhs=rows[:, tt, :], start=True, stop=True)
             else:
-                wt = state[("wt", i)]
+                zk, zm = state[("wt", i)]
                 for j in range(PACK):
-                    nc.tensor.transpose(wb[:, j, :], wt[:, j * P : (j + 1) * P], ident_f[:])
+                    cols = slice(j * P, (j + 1) * P)
+                    nc.tensor.matmul(
+                        out=wb[:, j, :], lhsT=zk[:, cols], rhs=ident_f[:], is_transpose=True, start=True, stop=False
+                    )
+                    nc.tensor.matmul(
+                        out=wb[:, j, :], lhsT=zm[:, cols], rhs=ident_f[:], is_transpose=True, start=False, stop=True
+                    )
             nc.vector.tensor_tensor(
                 out=gg[:, tt * P : (tt + 1) * P, :],
                 in0=u[:, :, tt * P : (tt + 1) * P].rearrange("p j t -> p t j"),
@@ -302,36 +308,37 @@ def tile_hydraattention_pb_t_kernel(tc, x, mask, W_q, b_q, kv_know, kv_mask, W_o
 
         with tc.manual_schedule():
             for s in range(N_CHUNKS + 7):
-                if live(s - 4):
-                    pieces(s - 4)
-                if live(s):
-                    regroup_x(s)
+                chain = factor_chain(s - 4) if live(s - 4) else []
                 for k in range(TILES):
                     if live(s - 7):
                         project_out(s - 7, k)
+                    if k < len(chain):
+                        chain[k]()
                     if live(s - 2):
                         project_q(s - 2, k)
                 if live(s - 7):
                     store(s - 7)
                 if live(s - 1):
                     quantise_x(s - 1)
+                if live(s):
+                    regroup_x(s)
                 for k in range(TILES):
                     if live(s - 3):
                         square_sum(s - 3, k)
                     if live(s - 5):
                         gate(s - 5, k)
+                    if TILES + k < len(chain):
+                        chain[TILES + k]()
                 if live(s - 3):
                     norm(s - 3)
-                if live(s - 5):
-                    quantise_g(s - 5)
                 if s == 1:
                     setup_mask()
                 if s == 2:
                     setup_kv()
                 if s == 3:
                     setup_out()
-                if live(s - 3):
-                    factors(s - 3)
+                if live(s - 5):
+                    quantise_g(s - 5)
                 if live(s - 4):
                     gate_last_tile(s - 4)
                     factor_rows(s - 4)

@@ -72,27 +72,18 @@ def tile_hydraattention_pb_t_kernel(tc, x, mask, W_q, b_q, kv_know, kv_mask, W_o
                 if b == 0 and k == 1:
                     nc.sync.dma_start(out=wo_raw[:], in_=W_out.rearrange("(p j) o -> p j o", j=PACK))
 
-        bq_raw = const.tile([P, PACK], BF16, name="bq_raw")
-        nc.scalar.dma_start(out=bq_raw[:], in_=b_q.rearrange("(p j) -> p j", j=PACK))
+        def load_vec4(vec, label):
+            raw = const.tile([P, PACK], BF16, name=label)
+            nc.scalar.dma_start(out=raw[:], in_=vec.rearrange("(p j) -> p j", j=PACK))
+            return raw
+
+        bq_raw = load_vec4(b_q, "bq_raw")
         m_raw = const.tile([P, P], BF16, name="m_raw")
         nc.vector.memset(m_raw[:], 0.0)
         nc.scalar.dma_start(out=m_raw[0:N_TILES, :], in_=mask.rearrange("b o (g h) w -> (b o g) (h w)", h=2))
-        l_full = []
-        kv_bc = []
-        for b in range(IMAGES):
-            lf = const.tile([P, C], BF16, name="l_full%d" % b)
-            nc.vector.memset(lf[:], 0.0)
-            nc.scalar.dma_start(out=lf[0:3, :], in_=kv_know[b, 0, :].partition_broadcast(3))
-            nc.scalar.dma_start(out=lf[3:6, :], in_=kv_mask[b, 0, :].partition_broadcast(3))
-            l_full.append(lf)
-        for b in range(IMAGES):
-            kb = const.tile([P, C], BF16, name="kkbc%d" % b)
-            nc.scalar.dma_start(out=kb[:], in_=kv_know[b, 0, :].partition_broadcast(P))
-            mb = const.tile([P, C], BF16, name="kmbc%d" % b)
-            nc.scalar.dma_start(out=mb[:], in_=kv_mask[b, 0, :].partition_broadcast(P))
-            kv_bc.append((kb, mb))
-        bo_raw = const.tile([P, C], BF16, name="bo_raw")
-        nc.scalar.dma_start(out=bo_raw[:], in_=b_out.partition_broadcast(P))
+        kk_raw = [load_vec4(kv_know[b, 0, :], "kk_raw%d" % b) for b in range(IMAGES)]
+        km_raw = [load_vec4(kv_mask[b, 0, :], "km_raw%d" % b) for b in range(IMAGES)]
+        bo_raw = load_vec4(b_out, "bo_raw")
 
         warm = const.tile([P, 1], F32, name="warm")
         nc.vector.memset(warm[:], 1.0)
@@ -102,7 +93,7 @@ def tile_hydraattention_pb_t_kernel(tc, x, mask, W_q, b_q, kv_know, kv_mask, W_o
         for k in range(2):
             nc.vector.memset(r_in[k][:], 0.0)
 
-        wq_grp = xgp.tile([P, C, PACK], BF16, name="wq_grp", tag="xg", align_bytes=64)
+        wq_grp = const.tile([P, C, PACK], BF16, name="wq_grp", align_bytes=64)
         nc.vector.tensor_copy(
             out=wq_grp[:].rearrange("q (j p) k -> q j p k", j=PACK),
             in_=wq_raw[:].rearrange("q k (p j) -> q j p k", j=PACK),
@@ -112,11 +103,45 @@ def tile_hydraattention_pb_t_kernel(tc, x, mask, W_q, b_q, kv_know, kv_mask, W_o
         )
         nc.vector.tensor_copy(out=bq4[:], in_=bq_raw[:])
 
-        def setup_mask():
-            m_ps = psum.tile([P, P], BF16, name="m_ps", tag="sd")
+        vec4 = {}
+        lin = [const.tile([P, PACK, P], BF16, name="lin%d" % b) for b in range(IMAGES)]
+        banks = {}
+
+        def prepare_constants():
+            for label, raw in (("kk0", kk_raw[0]), ("km0", km_raw[0]), ("kk1", kk_raw[1]), ("km1", km_raw[1]), ("bo", bo_raw)):
+                v4 = const.tile([P, PACK], F32, name="v4_" + label)
+                nc.vector.tensor_copy(out=v4[:], in_=raw[:])
+                vec4[label] = v4
+            for b in range(IMAGES):
+                nc.vector.memset(lin[b][:], 0.0)
+                nc.vector.tensor_copy(out=lin[b][:, :, 0:3], in_=kk_raw[b][:].unsqueeze(2).to_broadcast([P, PACK, 3]))
+                nc.vector.tensor_copy(out=lin[b][:, :, 3:6], in_=km_raw[b][:].unsqueeze(2).to_broadcast([P, PACK, 3]))
+
+        def spread(label):
+            ps = psum.tile([P, PACK, P], F32, name="spread_ps", tag="vd")
+            for j in range(PACK):
+                nc.tensor.transpose(ps[:, j, :], vec4[label][:, j : j + 1].to_broadcast([P, P]), ident_f[:])
+            banks[label] = ps
+
+        def transpose_rows(b):
+            lp = psum.tile([P, PACK, P], BF16, name="lp", tag="vd")
+            for j in range(PACK):
+                nc.tensor.transpose(lp[:, j, :], lin[b][:, j, :], ident_b[:])
+            banks["l%d" % b] = lp
+
+        def transpose_mask():
+            m_ps = psum.tile([P, P], BF16, name="m_ps", tag="vd")
             nc.tensor.transpose(m_ps[:], m_raw[:], ident_b[:])
+            banks["m"] = m_ps
+
+        def keep_kv(b):
+            nc.vector.tensor_copy(out=kk_b[b][:], in_=banks["kk%d" % b][:].rearrange("q j p -> q (j p)"))
+            nc.vector.tensor_copy(out=km_b[b][:], in_=banks["km%d" % b][:].rearrange("q j p -> q (j p)"))
+            nc.vector.tensor_copy(out=l_rows[b][:], in_=banks["l%d" % b][:])
+
+        def keep_mask():
             m_t = const.tile([P, N_TILES], F32, name="m_t")
-            nc.vector.tensor_copy(out=m_t[:], in_=m_ps[:, 0:N_TILES])
+            nc.vector.tensor_copy(out=m_t[:], in_=banks["m"][:, 0:N_TILES])
             inv = const.tile([P, N_TILES], F32, name="inv")
             nc.vector.tensor_scalar(out=inv[:], in0=m_t[:], scalar1=-1.0, scalar2=1.0, op0=ALU.mult, op1=ALU.add)
             mix = const.tile([P, N_TILES], F32, name="mix")
@@ -126,22 +151,12 @@ def tile_hydraattention_pb_t_kernel(tc, x, mask, W_q, b_q, kv_know, kv_mask, W_o
                 out=ab0[:, :, 1], in0=m_t[:], scalar=0.7, in1=m_t[:], op0=ALU.mult, op1=ALU.mult
             )
 
-        def setup_kv():
-            for b in range(IMAGES):
-                nc.vector.tensor_copy(out=l_rows[b][:], in_=l_full[b][:].rearrange("r (p j) -> r j p", j=PACK))
-                nc.vector.tensor_copy(
-                    out=kk_b[b][:].rearrange("q (j p) -> q j p", j=PACK),
-                    in_=kv_bc[b][0][:].rearrange("q (p j) -> q j p", j=PACK),
-                )
-                nc.vector.tensor_copy(
-                    out=km_b[b][:].rearrange("q (j p) -> q j p", j=PACK),
-                    in_=kv_bc[b][1][:].rearrange("q (p j) -> q j p", j=PACK),
-                )
-
-        def setup_out():
+        def keep_out():
             wo_grp = work.tile([P, C, PACK], BF16, name="wo_grp", tag="gg", align_bytes=64)
             nc.vector.tensor_copy(out=wo_grp[:], in_=wo_raw[:].rearrange("p j o -> p o j"))
-            nc.vector.tensor_copy(out=bo_b[:], in_=bo_raw[:])
+            nc.vector.tensor_copy(
+                out=bo_b[:].rearrange("q (p j) -> q p j", j=PACK), in_=banks["bo"][:].rearrange("q j p -> q p j")
+            )
             nc.vector.quantize_mx(
                 out=wo_codes[:].bitcast(FP8X4), scales=wo_sc[:], in_=wo_grp[:].rearrange("p o j -> p (o j)")
             )
@@ -308,6 +323,11 @@ def tile_hydraattention_pb_t_kernel(tc, x, mask, W_q, b_q, kv_know, kv_mask, W_o
 
         with tc.manual_schedule():
             for s in range(N_CHUNKS + 7):
+                if s == 1:
+                    transpose_mask()
+                    spread("kk0")
+                    spread("km0")
+                    transpose_rows(0)
                 chain = factor_chain(s - 4) if live(s - 4) else []
                 for k in range(TILES):
                     if live(s - 7):
@@ -322,6 +342,11 @@ def tile_hydraattention_pb_t_kernel(tc, x, mask, W_q, b_q, kv_know, kv_mask, W_o
                     quantise_x(s - 1)
                 if live(s):
                     regroup_x(s)
+                if s == 2:
+                    spread("kk1")
+                    spread("km1")
+                    transpose_rows(1)
+                    spread("bo")
                 for k in range(TILES):
                     if live(s - 3):
                         square_sum(s - 3, k)
@@ -331,12 +356,14 @@ def tile_hydraattention_pb_t_kernel(tc, x, mask, W_q, b_q, kv_know, kv_mask, W_o
                         chain[TILES + k]()
                 if live(s - 3):
                     norm(s - 3)
+                if s == 0:
+                    prepare_constants()
                 if s == 1:
-                    setup_mask()
+                    keep_mask()
+                    keep_kv(0)
                 if s == 2:
-                    setup_kv()
-                if s == 3:
-                    setup_out()
+                    keep_kv(1)
+                    keep_out()
                 if live(s - 5):
                     quantise_g(s - 5)
                 if live(s - 4):

@@ -268,25 +268,25 @@ def tile_hydraattention_pb_t_kernel(tc, x, mask, W_q, b_q, kv_know, kv_mask, W_o
             if tt == 0:
                 state[("gg", i)] = work.tile([P, CHUNK, PACK], BF16, name="gg", align_bytes=64)
             gg = state[("gg", i)]
-            wb = psum.tile([P, PACK, P], F32, name="wb", tag="vd")
+            wb = psum.tile([P, P, PACK], F32, name="wb", tag="vd")
             if tt < PE_TILES:
                 rows = state[("rows", i)]
                 for j in range(PACK):
-                    nc.tensor.matmul(out=wb[:, j, :], lhsT=l_rows[b][:, j, :], rhs=rows[:, tt, :], start=True, stop=True)
+                    nc.tensor.matmul(out=wb[:, :, j], lhsT=l_rows[b][:, j, :], rhs=rows[:, tt, :], start=True, stop=True)
             else:
                 zk, zm = state[("wt", i)]
                 for j in range(PACK):
                     cols = slice(j * P, (j + 1) * P)
                     nc.tensor.matmul(
-                        out=wb[:, j, :], lhsT=zk[:, cols], rhs=ident_f[:], is_transpose=True, start=True, stop=False
+                        out=wb[:, :, j], lhsT=zk[:, cols], rhs=ident_f[:], is_transpose=True, start=True, stop=False
                     )
                     nc.tensor.matmul(
-                        out=wb[:, j, :], lhsT=zm[:, cols], rhs=ident_f[:], is_transpose=True, start=False, stop=True
+                        out=wb[:, :, j], lhsT=zm[:, cols], rhs=ident_f[:], is_transpose=True, start=False, stop=True
                     )
             nc.vector.tensor_tensor(
                 out=gg[:, tt * P : (tt + 1) * P, :],
                 in0=u[:, :, tt * P : (tt + 1) * P].rearrange("p j t -> p t j"),
-                in1=wb[:].rearrange("p j t -> p t j"),
+                in1=wb[:],
                 op=ALU.mult,
             )
 

@@ -34,7 +34,7 @@ def tile_hydraattention_pb_t_kernel(tc, x, mask, W_q, b_q, kv_know, kv_mask, W_o
         xpool = ctx.enter_context(tc.tile_pool(name="xpool", bufs=1))
         psum = ctx.enter_context(tc.psum_pool(name="psum", bufs=4))
         xq = ctx.enter_context(tc.tile_pool(name="xq", bufs=3))
-        upool = ctx.enter_context(tc.tile_pool(name="upool", bufs=5))
+        upool = ctx.enter_context(tc.tile_pool(name="upool", bufs=6))
         small = ctx.enter_context(tc.tile_pool(name="small", bufs=3))
         work = ctx.enter_context(tc.tile_pool(name="work", bufs=2))
         gq = ctx.enter_context(tc.tile_pool(name="gq", bufs=3))
@@ -220,29 +220,30 @@ def tile_hydraattention_pb_t_kernel(tc, x, mask, W_q, b_q, kv_know, kv_mask, W_o
             nc.scalar.activation(out=nrm[:], in_=state[("n2", i)][:], func=ACT.Sqrt)
             state[("nrm", i)] = nrm
 
-        def factor_chain(i):
-            nrm = state[("nrm", i)]
+        def reciprocal_norm(i):
             rn = small.tile([P, TILES], F32, name="rn")
+            nc.vector.reciprocal(out=rn[:], in_=state[("nrm", i)][:])
+            state[("rn", i)] = rn
+
+        def factor_chain(i):
+            rn = state[("rn", i)]
             ab = small.tile([P, TILES, 2], F32, name="ab")
             r1 = small.tile([P, PE_TILES, 2], F32, name="r1")
             r2 = small.tile([P, PE_TILES, 2], F32, name="r2")
             rin = r_in[i % 2]
             head = ab[:, 0:PE_TILES, :]
             state[("ab", i)] = ab
-            return [
-                lambda: nc.vector.reciprocal(out=rn[:], in_=nrm[:]),
-                lambda: nc.vector.tensor_tensor(
-                    out=ab[:],
-                    in0=ab0[:, i * TILES : (i + 1) * TILES, :],
-                    in1=rn[:].unsqueeze(2).to_broadcast([P, TILES, 2]),
-                    op=ALU.mult,
-                ),
-                lambda: nc.vector.tensor_copy(out=rin[:, :, 0:6:3], in_=head),
-                lambda: nc.vector.tensor_tensor(out=r1[:], in0=head, in1=rin[:, :, 0:6:3], op=ALU.subtract),
-                lambda: nc.vector.tensor_copy(out=rin[:, :, 1:6:3], in_=r1[:]),
-                lambda: nc.vector.tensor_tensor(out=r2[:], in0=r1[:], in1=rin[:, :, 1:6:3], op=ALU.subtract),
-                lambda: nc.vector.tensor_copy(out=rin[:, :, 2:6:3], in_=r2[:]),
-            ]
+            nc.gpsimd.tensor_tensor(
+                out=ab[:],
+                in0=ab0[:, i * TILES : (i + 1) * TILES, :],
+                in1=rn[:].unsqueeze(2).to_broadcast([P, TILES, 2]),
+                op=ALU.mult,
+            )
+            nc.gpsimd.tensor_copy(out=rin[:, :, 0:6:3], in_=head)
+            nc.gpsimd.tensor_tensor(out=r1[:], in0=head, in1=rin[:, :, 0:6:3], op=ALU.subtract)
+            nc.gpsimd.tensor_copy(out=rin[:, :, 1:6:3], in_=r1[:])
+            nc.gpsimd.tensor_tensor(out=r2[:], in0=r1[:], in1=rin[:, :, 1:6:3], op=ALU.subtract)
+            nc.gpsimd.tensor_copy(out=rin[:, :, 2:6:3], in_=r2[:])
 
         def gate_last_tile(i):
             b = i // CHUNKS_PER_IMAGE
@@ -322,26 +323,29 @@ def tile_hydraattention_pb_t_kernel(tc, x, mask, W_q, b_q, kv_know, kv_mask, W_o
             )
 
         with tc.manual_schedule():
-            for s in range(N_CHUNKS + 7):
+            for s in range(N_CHUNKS + 9):
                 if s == 1:
                     transpose_mask()
                     spread("kk0")
                     spread("km0")
                     transpose_rows(0)
-                chain = factor_chain(s - 4) if live(s - 4) else []
                 for k in range(TILES):
-                    if live(s - 7):
-                        project_out(s - 7, k)
-                    if k < len(chain):
-                        chain[k]()
+                    if live(s - 8):
+                        project_out(s - 8, k)
                     if live(s - 2):
                         project_q(s - 2, k)
+                if live(s - 8):
+                    store(s - 8)
+                if live(s - 4):
+                    reciprocal_norm(s - 4)
                 if live(s - 7):
-                    store(s - 7)
+                    quantise_g(s - 7)
                 if live(s - 1):
                     quantise_x(s - 1)
                 if live(s):
                     regroup_x(s)
+                if live(s - 4):
+                    factor_chain(s - 4)
                 if s == 2:
                     spread("kk1")
                     spread("km1")
@@ -350,10 +354,8 @@ def tile_hydraattention_pb_t_kernel(tc, x, mask, W_q, b_q, kv_know, kv_mask, W_o
                 for k in range(TILES):
                     if live(s - 3):
                         square_sum(s - 3, k)
-                    if live(s - 5):
-                        gate(s - 5, k)
-                    if TILES + k < len(chain):
-                        chain[TILES + k]()
+                    if live(s - 6):
+                        gate(s - 6, k)
                 if live(s - 3):
                     norm(s - 3)
                 if s == 0:
@@ -365,7 +367,5 @@ def tile_hydraattention_pb_t_kernel(tc, x, mask, W_q, b_q, kv_know, kv_mask, W_o
                     keep_kv(1)
                     keep_out()
                 if live(s - 5):
-                    quantise_g(s - 5)
-                if live(s - 4):
-                    gate_last_tile(s - 4)
-                    factor_rows(s - 4)
+                    gate_last_tile(s - 5)
+                    factor_rows(s - 5)

@@ -330,10 +330,10 @@ def tile_hydraattention_pb_t_kernel(tc, x, mask, W_q, b_q, kv_know, kv_mask, W_o
                     spread("km0")
                     transpose_rows(0)
                 for k in range(TILES):
-                    if live(s - 8):
-                        project_out(s - 8, k)
                     if live(s - 2):
                         project_q(s - 2, k)
+                    if live(s - 8):
+                        project_out(s - 8, k)
                 if live(s - 8):
                     store(s - 8)
                 if live(s - 4):
@@ -346,16 +346,23 @@ def tile_hydraattention_pb_t_kernel(tc, x, mask, W_q, b_q, kv_know, kv_mask, W_o
                     regroup_x(s)
                 if live(s - 4):
                     factor_chain(s - 4)
+                if live(s - 5):
+                    gate_last_tile(s - 5)
+                if live(s - 6):
+                    for k in range(PE_TILES):
+                        gate(s - 6, k)
                 if s == 2:
                     spread("kk1")
                     spread("km1")
                     transpose_rows(1)
                     spread("bo")
-                for k in range(TILES):
-                    if live(s - 3):
+                if live(s - 3):
+                    for k in range(TILES):
                         square_sum(s - 3, k)
-                    if live(s - 6):
-                        gate(s - 6, k)
+                if live(s - 6):
+                    gate(s - 6, PE_TILES)
+                if live(s - 5):
+                    factor_rows(s - 5)
                 if live(s - 3):
                     norm(s - 3)
                 if s == 0:
@@ -366,6 +373,3 @@ def tile_hydraattention_pb_t_kernel(tc, x, mask, W_q, b_q, kv_know, kv_mask, W_o
                 if s == 2:
                     keep_kv(1)
                     keep_out()
-                if live(s - 5):
-                    gate_last_tile(s - 5)
-                    factor_rows(s - 5)

@@ -114,8 +114,8 @@ def tile_hydraattention_pb_t_kernel(tc, x, mask, W_q, b_q, kv_know, kv_mask, W_o
                 vec4[label] = v4
             for b in range(IMAGES):
                 nc.vector.memset(lin[b][:], 0.0)
-                nc.vector.tensor_copy(out=lin[b][:, :, 0:3], in_=kk_raw[b][:].unsqueeze(2).to_broadcast([P, PACK, 3]))
-                nc.vector.tensor_copy(out=lin[b][:, :, 3:6], in_=km_raw[b][:].unsqueeze(2).to_broadcast([P, PACK, 3]))
+                nc.vector.tensor_copy(out=lin[b][:, :, 0:4:2], in_=kk_raw[b][:].unsqueeze(2).to_broadcast([P, PACK, 2]))
+                nc.vector.tensor_copy(out=lin[b][:, :, 1:4:2], in_=km_raw[b][:].unsqueeze(2).to_broadcast([P, PACK, 2]))
 
         def spread(label):
             ps = psum.tile([P, PACK, P], F32, name="spread_ps", tag="vd")
@@ -228,10 +228,7 @@ def tile_hydraattention_pb_t_kernel(tc, x, mask, W_q, b_q, kv_know, kv_mask, W_o
         def factor_chain(i):
             rn = state[("rn", i)]
             ab = small.tile([P, TILES, 2], F32, name="ab")
-            r1 = small.tile([P, PE_TILES, 2], F32, name="r1")
-            r2 = small.tile([P, PE_TILES, 2], F32, name="r2")
             rin = r_in[i % 2]
-            head = ab[:, 0:PE_TILES, :]
             state[("ab", i)] = ab
             nc.gpsimd.tensor_tensor(
                 out=ab[:],
@@ -239,11 +236,13 @@ def tile_hydraattention_pb_t_kernel(tc, x, mask, W_q, b_q, kv_know, kv_mask, W_o
                 in1=rn[:].unsqueeze(2).to_broadcast([P, TILES, 2]),
                 op=ALU.mult,
             )
-            nc.gpsimd.tensor_copy(out=rin[:, :, 0:6:3], in_=head)
-            nc.gpsimd.tensor_tensor(out=r1[:], in0=head, in1=rin[:, :, 0:6:3], op=ALU.subtract)
-            nc.gpsimd.tensor_copy(out=rin[:, :, 1:6:3], in_=r1[:])
-            nc.gpsimd.tensor_tensor(out=r2[:], in0=r1[:], in1=rin[:, :, 1:6:3], op=ALU.subtract)
-            nc.gpsimd.tensor_copy(out=rin[:, :, 2:6:3], in_=r2[:])
+            nc.gpsimd.tensor_tensor(
+                out=rin[:, :, 0:2],
+                in0=ab0[:, i * TILES : i * TILES + PE_TILES, :],
+                in1=rn[:, 0:PE_TILES].unsqueeze(2).to_broadcast([P, PE_TILES, 2]),
+                op=ALU.mult,
+            )
+            nc.gpsimd.tensor_tensor(out=rin[:, :, 2:4], in0=ab[:, 0:PE_TILES, :], in1=rin[:, :, 0:2], op=ALU.subtract)
 
         def gate_last_tile(i):
             b = i // CHUNKS_PER_IMAGE

@@ -23,6 +23,8 @@ N_CHUNKS = IMAGES * CHUNKS_PER_IMAGE
 N_TILES = N_CHUNKS * TILES
 XLOAD = 1024
 PE_TILES = 3
+V_HELP_STEPS = 6
+V_REGROUPS = 3
 
 FLOPS = 2 * 2 * IMAGES * NPIX * C * C
 
@@ -90,8 +92,10 @@ def tile_hydraattention_pb_t_kernel(tc, x, mask, W_q, b_q, kv_know, kv_mask, W_o
         nc.scalar.activation(out=warm[:], in_=warm[:], func=ACT.Sqrt)
         make_identity(nc, ident_b[:])
         make_identity(nc, ident_f[:])
+        lin = [const.tile([P, PACK, P], BF16, name="lin%d" % b) for b in range(IMAGES)]
         for k in range(2):
             nc.vector.memset(r_in[k][:], 0.0)
+            nc.vector.memset(lin[k][:], 0.0)
 
         wq_grp = const.tile([P, C, PACK], BF16, name="wq_grp", align_bytes=64)
         nc.vector.tensor_copy(
@@ -101,64 +105,57 @@ def tile_hydraattention_pb_t_kernel(tc, x, mask, W_q, b_q, kv_know, kv_mask, W_o
         nc.vector.quantize_mx(
             out=wq_codes[:].bitcast(FP8X4), scales=wq_sc[:], in_=wq_grp[:].rearrange("q c k -> q (c k)")
         )
-        nc.vector.tensor_copy(out=bq4[:], in_=bq_raw[:])
 
+        nc.scalar.copy(out=bq4[:], in_=bq_raw[:])
         vec4 = {}
-        lin = [const.tile([P, PACK, P], BF16, name="lin%d" % b) for b in range(IMAGES)]
-        banks = {}
+        for label, raw in (("kk0", kk_raw[0]), ("km0", km_raw[0]), ("kk1", kk_raw[1]), ("km1", km_raw[1]), ("bo", bo_raw)):
+            v4 = const.tile([P, PACK], F32, name="v4_" + label)
+            nc.scalar.copy(out=v4[:], in_=raw[:])
+            vec4[label] = v4
+        for b in range(IMAGES):
+            nc.scalar.copy(out=lin[b][:, :, 0:4:2], in_=kk_raw[b][:].unsqueeze(2).to_broadcast([P, PACK, 2]))
+            nc.scalar.copy(out=lin[b][:, :, 1:4:2], in_=km_raw[b][:].unsqueeze(2).to_broadcast([P, PACK, 2]))
 
-        def prepare_constants():
-            for label, raw in (("kk0", kk_raw[0]), ("km0", km_raw[0]), ("kk1", kk_raw[1]), ("km1", km_raw[1]), ("bo", bo_raw)):
-                v4 = const.tile([P, PACK], F32, name="v4_" + label)
-                nc.vector.tensor_copy(out=v4[:], in_=raw[:])
-                vec4[label] = v4
-            for b in range(IMAGES):
-                nc.vector.memset(lin[b][:], 0.0)
-                nc.vector.tensor_copy(out=lin[b][:, :, 0:4:2], in_=kk_raw[b][:].unsqueeze(2).to_broadcast([P, PACK, 2]))
-                nc.vector.tensor_copy(out=lin[b][:, :, 1:4:2], in_=km_raw[b][:].unsqueeze(2).to_broadcast([P, PACK, 2]))
+        m_ps = psum.tile([P, P], BF16, name="m_ps", tag="sd")
+        nc.tensor.transpose(m_ps[:], m_raw[:], ident_b[:])
+        m_t = const.tile([P, N_TILES], F32, name="m_t")
+        nc.scalar.copy(out=m_t[:], in_=m_ps[:, 0:N_TILES])
+        inv = const.tile([P, N_TILES], F32, name="inv")
+        nc.gpsimd.tensor_scalar(out=inv[:], in0=m_t[:], scalar1=-1.0, scalar2=1.0, op0=ALU.mult, op1=ALU.add)
+        mix = const.tile([P, N_TILES], F32, name="mix")
+        nc.gpsimd.tensor_scalar(out=mix[:], in0=m_t[:], scalar1=-0.7, scalar2=1.0, op0=ALU.mult, op1=ALU.add)
+        m07 = const.tile([P, N_TILES], F32, name="m07")
+        nc.gpsimd.tensor_scalar(out=m07[:], in0=m_t[:], scalar1=0.7, scalar2=0.0, op0=ALU.mult, op1=ALU.add)
+        nc.gpsimd.tensor_tensor(out=ab0[:, :, 0], in0=inv[:], in1=mix[:], op=ALU.mult)
+        nc.gpsimd.tensor_tensor(out=ab0[:, :, 1], in0=m07[:], in1=m_t[:], op=ALU.mult)
 
-        def spread(label):
-            ps = psum.tile([P, PACK, P], F32, name="spread_ps", tag="vd")
+        def spread(label, tag):
+            ps = psum.tile([P, PACK, P], F32, name="spread_ps", tag=tag)
             for j in range(PACK):
                 nc.tensor.transpose(ps[:, j, :], vec4[label][:, j : j + 1].to_broadcast([P, P]), ident_f[:])
-            banks[label] = ps
+            return ps
 
-        def transpose_rows(b):
-            lp = psum.tile([P, PACK, P], BF16, name="lp", tag="vd")
+        for b in range(IMAGES):
+            tag = "vd" if b == 0 else "sd"
+            kk_ps = spread("kk%d" % b, tag)
+            nc.scalar.copy(out=kk_b[b][:], in_=kk_ps[:].rearrange("q j p -> q (j p)"))
+            km_ps = spread("km%d" % b, tag)
+            nc.scalar.copy(out=km_b[b][:], in_=km_ps[:].rearrange("q j p -> q (j p)"))
+            lp = psum.tile([P, PACK, P], BF16, name="lp", tag=tag)
             for j in range(PACK):
                 nc.tensor.transpose(lp[:, j, :], lin[b][:, j, :], ident_b[:])
-            banks["l%d" % b] = lp
+            nc.scalar.copy(out=l_rows[b][:], in_=lp[:])
+        bo_ps = spread("bo", "vd")
+        nc.scalar.copy(out=bo_b[:].rearrange("q (p j) -> q p j", j=PACK), in_=bo_ps[:].rearrange("q j p -> q p j"))
 
-        def transpose_mask():
-            m_ps = psum.tile([P, P], BF16, name="m_ps", tag="vd")
-            nc.tensor.transpose(m_ps[:], m_raw[:], ident_b[:])
-            banks["m"] = m_ps
-
-        def keep_kv(b):
-            nc.vector.tensor_copy(out=kk_b[b][:], in_=banks["kk%d" % b][:].rearrange("q j p -> q (j p)"))
-            nc.vector.tensor_copy(out=km_b[b][:], in_=banks["km%d" % b][:].rearrange("q j p -> q (j p)"))
-            nc.vector.tensor_copy(out=l_rows[b][:], in_=banks["l%d" % b][:])
-
-        def keep_mask():
-            m_t = const.tile([P, N_TILES], F32, name="m_t")
-            nc.vector.tensor_copy(out=m_t[:], in_=banks["m"][:, 0:N_TILES])
-            inv = const.tile([P, N_TILES], F32, name="inv")
-            nc.vector.tensor_scalar(out=inv[:], in0=m_t[:], scalar1=-1.0, scalar2=1.0, op0=ALU.mult, op1=ALU.add)
-            mix = const.tile([P, N_TILES], F32, name="mix")
-            nc.vector.scalar_tensor_tensor(out=mix[:], in0=m_t[:], scalar=0.3, in1=inv[:], op0=ALU.mult, op1=ALU.add)
-            nc.vector.tensor_tensor(out=ab0[:, :, 0], in0=inv[:], in1=mix[:], op=ALU.mult)
-            nc.vector.scalar_tensor_tensor(
-                out=ab0[:, :, 1], in0=m_t[:], scalar=0.7, in1=m_t[:], op0=ALU.mult, op1=ALU.mult
-            )
-
-        def keep_out():
+        def quantise_w_out():
             wo_grp = work.tile([P, C, PACK], BF16, name="wo_grp", tag="gg", align_bytes=64)
             nc.vector.tensor_copy(out=wo_grp[:], in_=wo_raw[:].rearrange("p j o -> p o j"))
-            nc.vector.tensor_copy(
-                out=bo_b[:].rearrange("q (p j) -> q p j", j=PACK), in_=banks["bo"][:].rearrange("q j p -> q p j")
-            )
+            state["wo_grp"] = wo_grp
+
+        def quantise_w_out2():
             nc.vector.quantize_mx(
-                out=wo_codes[:].bitcast(FP8X4), scales=wo_sc[:], in_=wo_grp[:].rearrange("p o j -> p (o j)")
+                out=wo_codes[:].bitcast(FP8X4), scales=wo_sc[:], in_=state["wo_grp"][:].rearrange("p o j -> p (o j)")
             )
 
         state = {}
@@ -170,14 +167,17 @@ def tile_hydraattention_pb_t_kernel(tc, x, mask, W_q, b_q, kv_know, kv_mask, W_o
             xr = x_raw[i // 2]
             off = (i % 2) * CHUNK
             xg = xgp.tile([P, CHUNK, PACK], BF16, name="xg", tag="xg", align_bytes=64)
-            nc.gpsimd.tensor_scalar(
-                out=xg[:],
-                in0=xr[:, :, off : off + CHUNK].rearrange("p j t -> p t j"),
-                scalar1=1.0,
-                scalar2=0.0,
-                op0=ALU.mult,
-                op1=ALU.add,
-            )
+            if i < V_REGROUPS:
+                nc.vector.tensor_copy(out=xg[:], in_=xr[:, :, off : off + CHUNK].rearrange("p j t -> p t j"))
+            else:
+                nc.gpsimd.tensor_scalar(
+                    out=xg[:],
+                    in0=xr[:, :, off : off + CHUNK].rearrange("p j t -> p t j"),
+                    scalar1=1.0,
+                    scalar2=0.0,
+                    op0=ALU.mult,
+                    op1=ALU.add,
+                )
             state[("xg", i)] = xg
 
         def quantise_x(i):
@@ -187,12 +187,12 @@ def tile_hydraattention_pb_t_kernel(tc, x, mask, W_q, b_q, kv_know, kv_mask, W_o
             nc.vector.quantize_mx(out=xc[:].bitcast(FP8X4), scales=xs[:], in_=xg[:].rearrange("p t j -> p (t j)"))
             state[("x", i)] = (xc, xs)
 
-        def project_q(i, j):
+        def project_q(i, j, by_vector):
             xc, xs = state[("x", i)]
             if j == 0:
                 state[("u", i)] = upool.tile([P, PACK, CHUNK], F32, name="u")
             u = state[("u", i)]
-            q = psum.tile([P, CHUNK], F32, name="q", tag="sd")
+            q = psum.tile([P, CHUNK], F32, name="q", tag="vd" if by_vector else "sd")
             nc.tensor.matmul_mx(
                 out=q[:],
                 lhsT=wq_codes[:, j * P : (j + 1) * P].bitcast(FP8X4),
@@ -202,7 +202,10 @@ def tile_hydraattention_pb_t_kernel(tc, x, mask, W_q, b_q, kv_know, kv_mask, W_o
                 start=True,
                 stop=True,
             )
-            nc.scalar.activation(out=u[:, j, :], in_=q[:], func=ACT.Identity, bias=bq4[:, j : j + 1], scale=1.0)
+            if by_vector:
+                nc.vector.tensor_scalar(out=u[:, j, :], in0=q[:], scalar1=bq4[:, j : j + 1], scalar2=None, op0=ALU.add)
+            else:
+                nc.scalar.activation(out=u[:, j, :], in_=q[:], func=ACT.Identity, bias=bq4[:, j : j + 1], scale=1.0)
 
         def square_sum(i, tt):
             u = state[("u", i)]
@@ -322,53 +325,37 @@ def tile_hydraattention_pb_t_kernel(tc, x, mask, W_q, b_q, kv_know, kv_mask, W_o
             )
 
         with tc.manual_schedule():
-            for s in range(N_CHUNKS + 9):
-                if s == 1:
-                    transpose_mask()
-                    spread("kk0")
-                    spread("km0")
-                    transpose_rows(0)
+            for s in range(N_CHUNKS + 8):
                 for k in range(TILES):
                     if live(s - 2):
-                        project_q(s - 2, k)
-                    if live(s - 8):
-                        project_out(s - 8, k)
-                if live(s - 8):
-                    store(s - 8)
+                        project_q(s - 2, k, s < V_HELP_STEPS and k % 2 == 1)
+                    if live(s - 7):
+                        project_out(s - 7, k)
+                    if k == 0 and live(s - 4):
+                        norm(s - 4)
+                if live(s - 7):
+                    store(s - 7)
                 if live(s - 4):
                     reciprocal_norm(s - 4)
-                if live(s - 7):
-                    quantise_g(s - 7)
+                    factor_chain(s - 4)
+                if live(s - 6):
+                    quantise_g(s - 6)
                 if live(s - 1):
                     quantise_x(s - 1)
                 if live(s):
                     regroup_x(s)
-                if live(s - 4):
-                    factor_chain(s - 4)
                 if live(s - 5):
-                    gate_last_tile(s - 5)
-                if live(s - 6):
                     for k in range(PE_TILES):
-                        gate(s - 6, k)
-                if s == 2:
-                    spread("kk1")
-                    spread("km1")
-                    transpose_rows(1)
-                    spread("bo")
+                        gate(s - 5, k)
                 if live(s - 3):
                     for k in range(TILES):
                         square_sum(s - 3, k)
-                if live(s - 6):
-                    gate(s - 6, PE_TILES)
                 if live(s - 5):
-                    factor_rows(s - 5)
-                if live(s - 3):
-                    norm(s - 3)
-                if s == 0:
-                    prepare_constants()
-                if s == 1:
-                    keep_mask()
-                    keep_kv(0)
+                    gate(s - 5, PE_TILES)
+                if live(s - 4):
+                    factor_rows(s - 4)
+                    gate_last_tile(s - 4)
                 if s == 2:
-                    keep_kv(1)
-                    keep_out()
+                    quantise_w_out()
+                if s == 3:
+                    quantise_w_out2()

@@ -287,9 +287,9 @@ def tile_hydraattention_pb_t_kernel(tc, x, mask, W_q, b_q, kv_know, kv_mask, W_o
                         out=wb[:, :, j], lhsT=zm[:, cols], rhs=ident_f[:], is_transpose=True, start=False, stop=True
                     )
             nc.vector.tensor_tensor(
-                out=gg[:, tt * P : (tt + 1) * P, :],
-                in0=u[:, :, tt * P : (tt + 1) * P].rearrange("p j t -> p t j"),
-                in1=wb[:],
+                out=gg[:, tt * P : (tt + 1) * P, :].rearrange("p (c i) j -> p c j i", i=PACK),
+                in0=u[:, :, tt * P : (tt + 1) * P].rearrange("p j (c i) -> p c j i", i=PACK),
+                in1=wb[:].rearrange("p (c i) j -> p c j i", i=PACK),
                 op=ALU.mult,
             )
 

@@ -331,13 +331,11 @@ def tile_hydraattention_pb_t_kernel(tc, x, mask, W_q, b_q, kv_know, kv_mask, W_o
                         project_q(s - 2, k, s < V_HELP_STEPS and k % 2 == 1)
                     if live(s - 7):
                         project_out(s - 7, k)
-                    if k == 0 and live(s - 4):
-                        norm(s - 4)
+                    if k == 1 and live(s - 4):
+                        reciprocal_norm(s - 4)
+                        factor_chain(s - 4)
                 if live(s - 7):
                     store(s - 7)
-                if live(s - 4):
-                    reciprocal_norm(s - 4)
-                    factor_chain(s - 4)
                 if live(s - 6):
                     quantise_g(s - 6)
                 if live(s - 1):
@@ -354,6 +352,9 @@ def tile_hydraattention_pb_t_kernel(tc, x, mask, W_q, b_q, kv_know, kv_mask, W_o
                     gate(s - 5, PE_TILES)
                 if live(s - 4):
                     factor_rows(s - 4)
+                if live(s - 3):
+                    norm(s - 3)
+                if live(s - 4):
                     gate_last_tile(s - 4)
                 if s == 2:
                     quantise_w_out()

@@ -271,25 +271,25 @@ def tile_hydraattention_pb_t_kernel(tc, x, mask, W_q, b_q, kv_know, kv_mask, W_o
             if tt == 0:
                 state[("gg", i)] = work.tile([P, CHUNK, PACK], BF16, name="gg", align_bytes=64)
             gg = state[("gg", i)]
-            wb = psum.tile([P, P, PACK], F32, name="wb", tag="vd")
+            wb = psum.tile([P, PACK, P], F32, name="wb", tag="vd")
             if tt < PE_TILES:
                 rows = state[("rows", i)]
                 for j in range(PACK):
-                    nc.tensor.matmul(out=wb[:, :, j], lhsT=l_rows[b][:, j, :], rhs=rows[:, tt, :], start=True, stop=True)
+                    nc.tensor.matmul(out=wb[:, j, :], lhsT=l_rows[b][:, j, :], rhs=rows[:, tt, :], start=True, stop=True)
             else:
                 zk, zm = state[("wt", i)]
                 for j in range(PACK):
                     cols = slice(j * P, (j + 1) * P)
                     nc.tensor.matmul(
-                        out=wb[:, :, j], lhsT=zk[:, cols], rhs=ident_f[:], is_transpose=True, start=True, stop=False
+                        out=wb[:, j, :], lhsT=zk[:, cols], rhs=ident_f[:], is_transpose=True, start=True, stop=False
                     )
                     nc.tensor.matmul(
-                        out=wb[:, :, j], lhsT=zm[:, cols], rhs=ident_f[:], is_transpose=True, start=False, stop=True
+                        out=wb[:, j, :], lhsT=zm[:, cols], rhs=ident_f[:], is_transpose=True, start=False, stop=True
                     )
             nc.vector.tensor_tensor(
                 out=gg[:, tt * P : (tt + 1) * P, :].rearrange("p (c i) j -> p c j i", i=PACK),
                 in0=u[:, :, tt * P : (tt + 1) * P].rearrange("p j (c i) -> p c j i", i=PACK),
-                in1=wb[:].rearrange("p (c i) j -> p c j i", i=PACK),
+                in1=wb[:].rearrange("p j (c i) -> p c j i", i=PACK),
                 op=ALU.mult,
             )
 

@@ -23,8 +23,8 @@ N_CHUNKS = IMAGES * CHUNKS_PER_IMAGE
 N_TILES = N_CHUNKS * TILES
 XLOAD = 1024
 PE_TILES = 3
-V_HELP_STEPS = 6
-V_REGROUPS = 3
+V_HELP_STEPS = 7
+V_REGROUPS = 5
 
 FLOPS = 2 * 2 * IMAGES * NPIX * C * C
 
@@ -150,7 +150,9 @@ def tile_hydraattention_pb_t_kernel(tc, x, mask, W_q, b_q, kv_know, kv_mask, W_o
 
         def quantise_w_out():
             wo_grp = work.tile([P, C, PACK], BF16, name="wo_grp", tag="gg", align_bytes=64)
-            nc.vector.tensor_copy(out=wo_grp[:], in_=wo_raw[:].rearrange("p j o -> p o j"))
+            nc.vector.tensor_copy(
+                out=wo_grp[:].rearrange("p (c i) j -> p c j i", i=PACK), in_=wo_raw[:].rearrange("p j (c i) -> p c j i", i=PACK)
+            )
             state["wo_grp"] = wo_grp
 
         def quantise_w_out2():
@@ -168,11 +170,14 @@ def tile_hydraattention_pb_t_kernel(tc, x, mask, W_q, b_q, kv_know, kv_mask, W_o
             off = (i % 2) * CHUNK
             xg = xgp.tile([P, CHUNK, PACK], BF16, name="xg", tag="xg", align_bytes=64)
             if i < V_REGROUPS:
-                nc.vector.tensor_copy(out=xg[:], in_=xr[:, :, off : off + CHUNK].rearrange("p j t -> p t j"))
+                nc.vector.tensor_copy(
+                    out=xg[:].rearrange("p (c i) j -> p c j i", i=PACK),
+                    in_=xr[:, :, off : off + CHUNK].rearrange("p j (c i) -> p c j i", i=PACK),
+                )
             else:
                 nc.gpsimd.tensor_scalar(
-                    out=xg[:],
-                    in0=xr[:, :, off : off + CHUNK].rearrange("p j t -> p t j"),
+                    out=xg[:].rearrange("p (c i) j -> p c j i", i=PACK),
+                    in0=xr[:, :, off : off + CHUNK].rearrange("p j (c i) -> p c j i", i=PACK),
                     scalar1=1.0,
                     scalar2=0.0,
                     op0=ALU.mult,
@@ -316,8 +321,14 @@ def tile_hydraattention_pb_t_kernel(tc, x, mask, W_q, b_q, kv_know, kv_mask, W_o
                 stop=True,
             )
             nc.vector.tensor_tensor(out=yo[:, tt, :], in0=y[:], in1=bo_b[:], op=ALU.add)
+            if i == N_CHUNKS - 1:
+                b = i // CHUNKS_PER_IMAGE
+                t0 = (i % CHUNKS_PER_IMAGE) * CHUNK + tt * P
+                nc.sync.dma_start(out=out[b, t0 : t0 + P, :], in_=yo[:, tt, :])
 
         def store(i):
+            if i == N_CHUNKS - 1:
+                return
             b = i // CHUNKS_PER_IMAGE
             t0 = (i % CHUNKS_PER_IMAGE) * CHUNK
             nc.sync.dma_start(

@@ -176,8 +176,8 @@ def tile_hydraattention_pb_t_kernel(tc, x, mask, W_q, b_q, kv_know, kv_mask, W_o
                 )
             else:
                 nc.gpsimd.tensor_scalar(
-                    out=xg[:].rearrange("p (c i) j -> p c j i", i=PACK),
-                    in0=xr[:, :, off : off + CHUNK].rearrange("p j (c i) -> p c j i", i=PACK),
+                    out=xg[:],
+                    in0=xr[:, :, off : off + CHUNK].rearrange("p j t -> p t j"),
                     scalar1=1.0,
                     scalar2=0.0,
                     op0=ALU.mult,

@@ -89,7 +89,7 @@ def tile_hydraattention_pb_t_kernel(tc, x, mask, W_q, b_q, kv_know, kv_mask, W_o
 
         warm = const.tile([P, 1], F32, name="warm")
         nc.vector.memset(warm[:], 1.0)
-        nc.scalar.activation(out=warm[:], in_=warm[:], func=ACT.Sqrt)
+        nc.scalar.activation(out=warm[:], in_=warm[:], func=ACT.Abs_reciprocal_sqrt)
         make_identity(nc, ident_b[:])
         make_identity(nc, ident_f[:])
         lin = [const.tile([P, PACK, P], BF16, name="lin%d" % b) for b in range(IMAGES)]
@@ -224,13 +224,8 @@ def tile_hydraattention_pb_t_kernel(tc, x, mask, W_q, b_q, kv_know, kv_mask, W_o
             nc.scalar.activation(out=junk[:], in_=ut[:], func=ACT.Square, accum_out=n2[:, tt : tt + 1])
 
         def norm(i):
-            nrm = small.tile([P, TILES], F32, name="nrm")
-            nc.scalar.activation(out=nrm[:], in_=state[("n2", i)][:], func=ACT.Sqrt)
-            state[("nrm", i)] = nrm
-
-        def reciprocal_norm(i):
             rn = small.tile([P, TILES], F32, name="rn")
-            nc.vector.reciprocal(out=rn[:], in_=state[("nrm", i)][:])
+            nc.scalar.activation(out=rn[:], in_=state[("n2", i)][:], func=ACT.Abs_reciprocal_sqrt)
             state[("rn", i)] = rn
 
         def factor_chain(i):
@@ -343,7 +338,6 @@ def tile_hydraattention_pb_t_kernel(tc, x, mask, W_q, b_q, kv_know, kv_mask, W_o
                     if live(s - 7):
                         project_out(s - 7, k)
                     if k == 1 and live(s - 4):
-                        reciprocal_norm(s - 4)
                         factor_chain(s - 4)
                 if live(s - 7):
                     store(s - 7)

@@ -22,9 +22,20 @@ CHUNKS_PER_IMAGE = NPIX // CHUNK
 N_CHUNKS = IMAGES * CHUNKS_PER_IMAGE
 N_TILES = N_CHUNKS * TILES
 XLOAD = 1024
-PE_TILES = 3
+PE_FULL_CHUNKS = 3
 V_HELP_STEPS = 7
 V_REGROUPS = 5
+S_BANK_FIRST = 11
+S_BANK_LAST = 14
+G_KNOW_FIRST = 12
+
+def pe_tiles(i):
+    return TILES if i < PE_FULL_CHUNKS else TILES - 1
+
+
+def scalar_empties_y(i, tt):
+    return S_BANK_FIRST <= i <= S_BANK_LAST and tt % 2 == 0
+
 
 FLOPS = 2 * 2 * IMAGES * NPIX * C * C
 
@@ -55,7 +66,7 @@ def tile_hydraattention_pb_t_kernel(tc, x, mask, W_q, b_q, kv_know, kv_mask, W_o
         l_rows = [const.tile([P, PACK, P], BF16, name="l_rows%d" % b) for b in range(IMAGES)]
         kk_b = [const.tile([P, C], F32, name="kk_b%d" % b) for b in range(IMAGES)]
         km_b = [const.tile([P, C], F32, name="km_b%d" % b) for b in range(IMAGES)]
-        r_in = [const.tile([P, PE_TILES, P], BF16, name="r_in%d" % k) for k in range(2)]
+        r_in = [const.tile([P, TILES, P], BF16, name="r_in%d" % k) for k in range(2)]
 
         wq_raw = work.tile([P, PACK, C], BF16, name="wq_raw", tag="gg", align_bytes=64)
         nc.sync.dma_start(out=wq_raw[:], in_=W_q.rearrange("(p j) c -> p j c", j=PACK))
@@ -240,29 +251,35 @@ def tile_hydraattention_pb_t_kernel(tc, x, mask, W_q, b_q, kv_know, kv_mask, W_o
                 op=ALU.mult,
             )
             nc.gpsimd.tensor_tensor(
-                out=rin[:, :, 0:2],
-                in0=ab0[:, i * TILES : i * TILES + PE_TILES, :],
-                in1=rn[:, 0:PE_TILES].unsqueeze(2).to_broadcast([P, PE_TILES, 2]),
+                out=rin[:, 0 : pe_tiles(i), 0:2],
+                in0=ab0[:, i * TILES : i * TILES + pe_tiles(i), :],
+                in1=rn[:, 0 : pe_tiles(i)].unsqueeze(2).to_broadcast([P, pe_tiles(i), 2]),
                 op=ALU.mult,
             )
-            nc.gpsimd.tensor_tensor(out=rin[:, :, 2:4], in0=ab[:, 0:PE_TILES, :], in1=rin[:, :, 0:2], op=ALU.subtract)
+            nc.gpsimd.tensor_tensor(out=rin[:, 0 : pe_tiles(i), 2:4], in0=ab[:, 0 : pe_tiles(i), :], in1=rin[:, 0 : pe_tiles(i), 0:2], op=ALU.subtract)
+
+        def scale_row(out_t, in_t, factor, on_g):
+            if on_g:
+                nc.gpsimd.tensor_scalar(out=out_t[:], in0=in_t[:], scalar1=factor, scalar2=0.0, op0=ALU.mult, op1=ALU.add)
+            else:
+                nc.scalar.activation(out=out_t[:], in_=in_t[:], func=ACT.Copy, scale=factor)
 
         def gate_last_tile(i):
             b = i // CHUNKS_PER_IMAGE
             ab = state[("ab", i)]
             zk = work.tile([P, C], F32, name="zk")
-            nc.scalar.activation(out=zk[:], in_=kk_b[b][:], func=ACT.Copy, scale=ab[:, PE_TILES, 0:1])
+            scale_row(zk, kk_b[b], ab[:, pe_tiles(i), 0:1], i >= G_KNOW_FIRST)
             zm = work.tile([P, C], F32, name="zm")
-            nc.scalar.activation(out=zm[:], in_=km_b[b][:], func=ACT.Copy, scale=ab[:, PE_TILES, 1:2])
+            scale_row(zm, km_b[b], ab[:, pe_tiles(i), 1:2], True)
             state[("wt", i)] = (zk, zm)
 
         def factor_rows(i):
             rin = r_in[i % 2]
-            rp = psum.tile([P, PE_TILES, P], BF16, name="rp", tag="sd")
-            for tt in range(PE_TILES):
+            rp = psum.tile([P, TILES, P], BF16, name="rp", tag="sd")
+            for tt in range(pe_tiles(i)):
                 nc.tensor.transpose(rp[:, tt, :], rin[:, tt, :], ident_b[:])
-            rows = work.tile([P, PE_TILES, P], BF16, name="rows")
-            nc.scalar.copy(out=rows[:], in_=rp[:])
+            rows = work.tile([P, TILES, P], BF16, name="rows")
+            nc.scalar.copy(out=rows[:, 0 : pe_tiles(i), :], in_=rp[:, 0 : pe_tiles(i), :])
             state[("rows", i)] = rows
 
         def gate(i, tt):
@@ -272,7 +289,7 @@ def tile_hydraattention_pb_t_kernel(tc, x, mask, W_q, b_q, kv_know, kv_mask, W_o
                 state[("gg", i)] = work.tile([P, CHUNK, PACK], BF16, name="gg", align_bytes=64)
             gg = state[("gg", i)]
             wb = psum.tile([P, PACK, P], F32, name="wb", tag="vd")
-            if tt < PE_TILES:
+            if tt < pe_tiles(i):
                 rows = state[("rows", i)]
                 for j in range(PACK):
                     nc.tensor.matmul(out=wb[:, j, :], lhsT=l_rows[b][:, j, :], rhs=rows[:, tt, :], start=True, stop=True)
@@ -305,7 +322,7 @@ def tile_hydraattention_pb_t_kernel(tc, x, mask, W_q, b_q, kv_know, kv_mask, W_o
             if tt == 0:
                 state[("yo", i)] = ypool.tile([P, TILES, C], F32, name="yo")
             yo = state[("yo", i)]
-            y = psum.tile([P, C], F32, name="y", tag="vd")
+            y = psum.tile([P, C], F32, name="y", tag="sd" if scalar_empties_y(i, tt) else "vd")
             nc.tensor.matmul_mx(
                 out=y[:],
                 lhsT=gc[:, tt * P : (tt + 1) * P].bitcast(FP8X4),
@@ -315,7 +332,11 @@ def tile_hydraattention_pb_t_kernel(tc, x, mask, W_q, b_q, kv_know, kv_mask, W_o
                 start=True,
                 stop=True,
             )
-            nc.vector.tensor_tensor(out=yo[:, tt, :], in0=y[:], in1=bo_b[:], op=ALU.add)
+            if scalar_empties_y(i, tt):
+                nc.scalar.copy(out=yo[:, tt, :], in_=y[:])
+                nc.gpsimd.tensor_tensor(out=yo[:, tt, :], in0=yo[:, tt, :], in1=bo_b[:], op=ALU.add)
+            else:
+                nc.vector.tensor_tensor(out=yo[:, tt, :], in0=y[:], in1=bo_b[:], op=ALU.add)
             if i == N_CHUNKS - 1:
                 b = i // CHUNKS_PER_IMAGE
                 t0 = (i % CHUNKS_PER_IMAGE) * CHUNK + tt * P
@@ -348,18 +369,18 @@ def tile_hydraattention_pb_t_kernel(tc, x, mask, W_q, b_q, kv_know, kv_mask, W_o
                 if live(s):
                     regroup_x(s)
                 if live(s - 5):
-                    for k in range(PE_TILES):
+                    for k in range(3):
                         gate(s - 5, k)
                 if live(s - 3):
                     for k in range(TILES):
                         square_sum(s - 3, k)
                 if live(s - 5):
-                    gate(s - 5, PE_TILES)
+                    gate(s - 5, 3)
                 if live(s - 4):
                     factor_rows(s - 4)
                 if live(s - 3):
                     norm(s - 3)
-                if live(s - 4):
+                if live(s - 4) and pe_tiles(s - 4) < 4:
                     gate_last_tile(s - 4)
                 if s == 2:
                     quantise_w_out()

@@ -22,19 +22,23 @@ CHUNKS_PER_IMAGE = NPIX // CHUNK
 N_CHUNKS = IMAGES * CHUNKS_PER_IMAGE
 N_TILES = N_CHUNKS * TILES
 XLOAD = 1024
-PE_FULL_CHUNKS = 3
 V_HELP_STEPS = 7
 V_REGROUPS = 5
+PE_FULL_CHUNKS = 3
 S_BANK_FIRST = 11
 S_BANK_LAST = 14
-G_KNOW_FIRST = 12
+
 
 def pe_tiles(i):
     return TILES if i < PE_FULL_CHUNKS else TILES - 1
 
 
 def scalar_empties_y(i, tt):
-    return S_BANK_FIRST <= i <= S_BANK_LAST and tt % 2 == 0
+    return S_BANK_FIRST <= i <= S_BANK_LAST and tt == 0
+
+
+def vector_empties_q(i, j):
+    return i + 2 < V_HELP_STEPS and j % 2 == 1
 
 
 FLOPS = 2 * 2 * IMAGES * NPIX * C * C
@@ -161,7 +165,7 @@ def tile_hydraattention_pb_t_kernel(tc, x, mask, W_q, b_q, kv_know, kv_mask, W_o
 
         def quantise_w_out():
             wo_grp = work.tile([P, C, PACK], BF16, name="wo_grp", tag="gg", align_bytes=64)
-            nc.vector.tensor_copy(
+            nc.scalar.copy(
                 out=wo_grp[:].rearrange("p (c i) j -> p c j i", i=PACK), in_=wo_raw[:].rearrange("p j (c i) -> p c j i", i=PACK)
             )
             state["wo_grp"] = wo_grp
@@ -203,12 +207,9 @@ def tile_hydraattention_pb_t_kernel(tc, x, mask, W_q, b_q, kv_know, kv_mask, W_o
             nc.vector.quantize_mx(out=xc[:].bitcast(FP8X4), scales=xs[:], in_=xg[:].rearrange("p t j -> p (t j)"))
             state[("x", i)] = (xc, xs)
 
-        def project_q(i, j, by_vector):
+        def project_q(i, j):
             xc, xs = state[("x", i)]
-            if j == 0:
-                state[("u", i)] = upool.tile([P, PACK, CHUNK], F32, name="u")
-            u = state[("u", i)]
-            q = psum.tile([P, CHUNK], F32, name="q", tag="vd" if by_vector else "sd")
+            q = psum.tile([P, CHUNK], F32, name="q", tag="vd" if vector_empties_q(i, j) else "sd")
             nc.tensor.matmul_mx(
                 out=q[:],
                 lhsT=wq_codes[:, j * P : (j + 1) * P].bitcast(FP8X4),
@@ -218,19 +219,30 @@ def tile_hydraattention_pb_t_kernel(tc, x, mask, W_q, b_q, kv_know, kv_mask, W_o
                 start=True,
                 stop=True,
             )
-            if by_vector:
+            state[("q", i, j)] = q
+
+        def empty_q(i, j):
+            if j == 0:
+                state[("u", i)] = upool.tile([P, PACK, CHUNK], F32, name="u")
+            u = state[("u", i)]
+            q = state[("q", i, j)]
+            if vector_empties_q(i, j):
                 nc.vector.tensor_scalar(out=u[:, j, :], in0=q[:], scalar1=bq4[:, j : j + 1], scalar2=None, op0=ALU.add)
             else:
                 nc.scalar.activation(out=u[:, j, :], in_=q[:], func=ACT.Identity, bias=bq4[:, j : j + 1], scale=1.0)
 
-        def square_sum(i, tt):
+        def pixel_rows(i, tt):
             u = state[("u", i)]
-            if tt == 0:
-                state[("n2", i)] = small.tile([P, TILES], F32, name="n2")
-            n2 = state[("n2", i)]
             ut = psum.tile([P, C], F32, name="ut", tag="sd")
             for j in range(PACK):
                 nc.tensor.transpose(ut[:, j * P : (j + 1) * P], u[:, j, tt * P : (tt + 1) * P], ident_f[:])
+            state[("ut", i, tt)] = ut
+
+        def square_sum(i, tt):
+            if tt == 0:
+                state[("n2", i)] = small.tile([P, TILES], F32, name="n2")
+            n2 = state[("n2", i)]
+            ut = state[("ut", i, tt)]
             junk = work.tile([P, C], BF16, name="junk")
             nc.scalar.activation(out=junk[:], in_=ut[:], func=ACT.Square, accum_out=n2[:, tt : tt + 1])
 
@@ -265,10 +277,12 @@ def tile_hydraattention_pb_t_kernel(tc, x, mask, W_q, b_q, kv_know, kv_mask, W_o
                 nc.scalar.activation(out=out_t[:], in_=in_t[:], func=ACT.Copy, scale=factor)
 
         def gate_last_tile(i):
+            if pe_tiles(i) == TILES:
+                return
             b = i // CHUNKS_PER_IMAGE
             ab = state[("ab", i)]
             zk = work.tile([P, C], F32, name="zk")
-            scale_row(zk, kk_b[b], ab[:, pe_tiles(i), 0:1], i >= G_KNOW_FIRST)
+            scale_row(zk, kk_b[b], ab[:, pe_tiles(i), 0:1], False)
             zm = work.tile([P, C], F32, name="zm")
             scale_row(zm, km_b[b], ab[:, pe_tiles(i), 1:2], True)
             state[("wt", i)] = (zk, zm)
@@ -282,12 +296,8 @@ def tile_hydraattention_pb_t_kernel(tc, x, mask, W_q, b_q, kv_know, kv_mask, W_o
             nc.scalar.copy(out=rows[:, 0 : pe_tiles(i), :], in_=rp[:, 0 : pe_tiles(i), :])
             state[("rows", i)] = rows
 
-        def gate(i, tt):
+        def gate_factor(i, tt):
             b = i // CHUNKS_PER_IMAGE
-            u = state[("u", i)]
-            if tt == 0:
-                state[("gg", i)] = work.tile([P, CHUNK, PACK], BF16, name="gg", align_bytes=64)
-            gg = state[("gg", i)]
             wb = psum.tile([P, PACK, P], F32, name="wb", tag="vd")
             if tt < pe_tiles(i):
                 rows = state[("rows", i)]
@@ -303,6 +313,14 @@ def tile_hydraattention_pb_t_kernel(tc, x, mask, W_q, b_q, kv_know, kv_mask, W_o
                     nc.tensor.matmul(
                         out=wb[:, j, :], lhsT=zm[:, cols], rhs=ident_f[:], is_transpose=True, start=False, stop=True
                     )
+            state[("wb", i, tt)] = wb
+
+        def gate(i, tt):
+            u = state[("u", i)]
+            if tt == 0:
+                state[("gg", i)] = work.tile([P, CHUNK, PACK], BF16, name="gg", align_bytes=64)
+            gg = state[("gg", i)]
+            wb = state[("wb", i, tt)]
             nc.vector.tensor_tensor(
                 out=gg[:, tt * P : (tt + 1) * P, :].rearrange("p (c i) j -> p c j i", i=PACK),
                 in0=u[:, :, tt * P : (tt + 1) * P].rearrange("p j (c i) -> p c j i", i=PACK),
@@ -319,9 +337,6 @@ def tile_hydraattention_pb_t_kernel(tc, x, mask, W_q, b_q, kv_know, kv_mask, W_o
 
         def project_out(i, tt):
             gc, gs = state[("g", i)]
-            if tt == 0:
-                state[("yo", i)] = ypool.tile([P, TILES, C], F32, name="yo")
-            yo = state[("yo", i)]
             y = psum.tile([P, C], F32, name="y", tag="sd" if scalar_empties_y(i, tt) else "vd")
             nc.tensor.matmul_mx(
                 out=y[:],
@@ -332,11 +347,27 @@ def tile_hydraattention_pb_t_kernel(tc, x, mask, W_q, b_q, kv_know, kv_mask, W_o
                 start=True,
                 stop=True,
             )
+            state[("y", i, tt)] = y
+
+        def empty_y(i, tt):
+            if tt == 0:
+                state[("yo", i)] = ypool.tile([P, TILES, C], F32, name="yo")
+            yo = state[("yo", i)]
+            y = state[("y", i, tt)]
             if scalar_empties_y(i, tt):
                 nc.scalar.copy(out=yo[:, tt, :], in_=y[:])
-                nc.gpsimd.tensor_tensor(out=yo[:, tt, :], in0=yo[:, tt, :], in1=bo_b[:], op=ALU.add)
             else:
                 nc.vector.tensor_tensor(out=yo[:, tt, :], in0=y[:], in1=bo_b[:], op=ALU.add)
+                store_tile(i, tt)
+
+        def add_y(i, tt):
+            yo = state[("yo", i)]
+            if scalar_empties_y(i, tt):
+                nc.gpsimd.tensor_tensor(out=yo[:, tt, :], in0=yo[:, tt, :], in1=bo_b[:], op=ALU.add)
+                store_tile(i, tt)
+
+        def store_tile(i, tt):
+            yo = state[("yo", i)]
             if i == N_CHUNKS - 1:
                 b = i // CHUNKS_PER_IMAGE
                 t0 = (i % CHUNKS_PER_IMAGE) * CHUNK + tt * P
@@ -353,15 +384,32 @@ def tile_hydraattention_pb_t_kernel(tc, x, mask, W_q, b_q, kv_know, kv_mask, W_o
 
         with tc.manual_schedule():
             for s in range(N_CHUNKS + 8):
-                for k in range(TILES):
-                    if live(s - 2):
-                        project_q(s - 2, k, s < V_HELP_STEPS and k % 2 == 1)
-                    if live(s - 7):
-                        project_out(s - 7, k)
-                    if k == 1 and live(s - 4):
-                        factor_chain(s - 4)
+                if live(s - 2):
+                    project_q(s - 2, 0)
+                    empty_q(s - 2, 0)
                 if live(s - 7):
-                    store(s - 7)
+                    project_out(s - 7, 0)
+                    empty_y(s - 7, 0)
+                if live(s - 2):
+                    project_q(s - 2, 1)
+                    empty_q(s - 2, 1)
+                if live(s - 7):
+                    project_out(s - 7, 1)
+                    empty_y(s - 7, 1)
+                if live(s - 4):
+                    factor_chain(s - 4)
+                if live(s - 2):
+                    project_q(s - 2, 2)
+                    empty_q(s - 2, 2)
+                if live(s - 7):
+                    project_out(s - 7, 2)
+                    empty_y(s - 7, 2)
+                if live(s - 2):
+                    project_q(s - 2, 3)
+                    empty_q(s - 2, 3)
+                if live(s - 7):
+                    project_out(s - 7, 3)
+                    empty_y(s - 7, 3)
                 if live(s - 6):
                     quantise_g(s - 6)
                 if live(s - 1):
@@ -369,19 +417,36 @@ def tile_hydraattention_pb_t_kernel(tc, x, mask, W_q, b_q, kv_know, kv_mask, W_o
                 if live(s):
                     regroup_x(s)
                 if live(s - 5):
-                    for k in range(3):
-                        gate(s - 5, k)
+                    gate_factor(s - 5, 0)
+                    gate(s - 5, 0)
+                    gate_factor(s - 5, 1)
+                    gate(s - 5, 1)
+                    gate_factor(s - 5, 2)
+                    gate(s - 5, 2)
                 if live(s - 3):
-                    for k in range(TILES):
-                        square_sum(s - 3, k)
+                    pixel_rows(s - 3, 0)
+                    square_sum(s - 3, 0)
+                    pixel_rows(s - 3, 1)
+                    square_sum(s - 3, 1)
+                    pixel_rows(s - 3, 2)
+                    square_sum(s - 3, 2)
+                    pixel_rows(s - 3, 3)
+                    square_sum(s - 3, 3)
                 if live(s - 5):
+                    gate_factor(s - 5, 3)
                     gate(s - 5, 3)
                 if live(s - 4):
                     factor_rows(s - 4)
                 if live(s - 3):
                     norm(s - 3)
-                if live(s - 4) and pe_tiles(s - 4) < 4:
+                if live(s - 4):
                     gate_last_tile(s - 4)
+                if live(s - 7):
+                    add_y(s - 7, 0)
+                    add_y(s - 7, 1)
+                    add_y(s - 7, 2)
+                    add_y(s - 7, 3)
+                    store(s - 7)
                 if s == 2:
                     quantise_w_out()
                 if s == 3:

@@ -22,6 +22,7 @@ CHUNKS_PER_IMAGE = NPIX // CHUNK
 N_CHUNKS = IMAGES * CHUNKS_PER_IMAGE
 N_TILES = N_CHUNKS * TILES
 XLOAD = 1024
+WALK = 2
 V_HELP_STEPS = 7
 V_REGROUPS = 5
 PE_FULL_CHUNKS = 3
@@ -322,9 +323,9 @@ def tile_hydraattention_pb_t_kernel(tc, x, mask, W_q, b_q, kv_know, kv_mask, W_o
             gg = state[("gg", i)]
             wb = state[("wb", i, tt)]
             nc.vector.tensor_tensor(
-                out=gg[:, tt * P : (tt + 1) * P, :].rearrange("p (c i) j -> p c j i", i=PACK),
-                in0=u[:, :, tt * P : (tt + 1) * P].rearrange("p j (c i) -> p c j i", i=PACK),
-                in1=wb[:].rearrange("p j (c i) -> p c j i", i=PACK),
+                out=gg[:, tt * P : (tt + 1) * P, :].rearrange("p (c i) j -> p c j i", i=WALK),
+                in0=u[:, :, tt * P : (tt + 1) * P].rearrange("p j (c i) -> p c j i", i=WALK),
+                in1=wb[:].rearrange("p j (c i) -> p c j i", i=WALK),
                 op=ALU.mult,
             )
 

@@ -66,11 +66,11 @@ def tile_hydraattention_pb_t_kernel(tc, x, mask, W_q, b_q, kv_know, kv_mask, W_o
         ident_f = const.tile([P, P], F32, name="ident_f")
         ident_b = const.tile([P, P], BF16, name="ident_b")
         bq4 = const.tile([P, PACK], F32, name="bq4")
-        bo_b = const.tile([P, C], F32, name="bo_b")
+        bo_b = const.tile([P, C], BF16, name="bo_b")
         ab0 = const.tile([P, N_TILES, 2], F32, name="ab0")
         l_rows = [const.tile([P, PACK, P], BF16, name="l_rows%d" % b) for b in range(IMAGES)]
-        kk_b = [const.tile([P, C], F32, name="kk_b%d" % b) for b in range(IMAGES)]
-        km_b = [const.tile([P, C], F32, name="km_b%d" % b) for b in range(IMAGES)]
+        kk_b = [const.tile([P, C], BF16, name="kk_b%d" % b) for b in range(IMAGES)]
+        km_b = [const.tile([P, C], BF16, name="km_b%d" % b) for b in range(IMAGES)]
         r_in = [const.tile([P, TILES, P], BF16, name="r_in%d" % k) for k in range(2)]
 
         wq_raw = work.tile([P, PACK, C], BF16, name="wq_raw", tag="gg", align_bytes=64)
@@ -90,18 +90,17 @@ def tile_hydraattention_pb_t_kernel(tc, x, mask, W_q, b_q, kv_know, kv_mask, W_o
                 if b == 0 and k == 1:
                     nc.sync.dma_start(out=wo_raw[:], in_=W_out.rearrange("(p j) o -> p j o", j=PACK))
 
-        def load_vec4(vec, label):
-            raw = const.tile([P, PACK], BF16, name=label)
-            nc.scalar.dma_start(out=raw[:], in_=vec.rearrange("(p j) -> p j", j=PACK))
-            return raw
-
-        bq_raw = load_vec4(b_q, "bq_raw")
+        bq_raw = const.tile([P, PACK], BF16, name="bq_raw")
+        nc.scalar.dma_start(out=bq_raw[:], in_=b_q.rearrange("(p j) -> p j", j=PACK))
+        kk_raw = const.tile([P, IMAGES, PACK], BF16, name="kk_raw")
+        nc.scalar.dma_start(out=kk_raw[:], in_=kv_know.rearrange("b o (p j) -> p (b o) j", j=PACK))
+        km_raw = const.tile([P, IMAGES, PACK], BF16, name="km_raw")
+        nc.scalar.dma_start(out=km_raw[:], in_=kv_mask.rearrange("b o (p j) -> p (b o) j", j=PACK))
+        bo_raw = const.tile([P, PACK], BF16, name="bo_raw")
+        nc.scalar.dma_start(out=bo_raw[:], in_=b_out.rearrange("(p j) -> p j", j=PACK))
         m_raw = const.tile([P, P], BF16, name="m_raw")
         nc.vector.memset(m_raw[:], 0.0)
         nc.scalar.dma_start(out=m_raw[0:N_TILES, :], in_=mask.rearrange("b o (g h) w -> (b o g) (h w)", h=2))
-        kk_raw = [load_vec4(kv_know[b, 0, :], "kk_raw%d" % b) for b in range(IMAGES)]
-        km_raw = [load_vec4(kv_mask[b, 0, :], "km_raw%d" % b) for b in range(IMAGES)]
-        bo_raw = load_vec4(b_out, "bo_raw")
 
         warm = const.tile([P, 1], F32, name="warm")
         nc.vector.memset(warm[:], 1.0)
@@ -123,14 +122,28 @@ def tile_hydraattention_pb_t_kernel(tc, x, mask, W_q, b_q, kv_know, kv_mask, W_o
         )
 
         nc.scalar.copy(out=bq4[:], in_=bq_raw[:])
-        vec4 = {}
-        for label, raw in (("kk0", kk_raw[0]), ("km0", km_raw[0]), ("kk1", kk_raw[1]), ("km1", km_raw[1]), ("bo", bo_raw)):
-            v4 = const.tile([P, PACK], F32, name="v4_" + label)
-            nc.scalar.copy(out=v4[:], in_=raw[:])
-            vec4[label] = v4
         for b in range(IMAGES):
-            nc.scalar.copy(out=lin[b][:, :, 0:4:2], in_=kk_raw[b][:].unsqueeze(2).to_broadcast([P, PACK, 2]))
-            nc.scalar.copy(out=lin[b][:, :, 1:4:2], in_=km_raw[b][:].unsqueeze(2).to_broadcast([P, PACK, 2]))
+            nc.scalar.copy(out=lin[b][:, :, 0:4:2], in_=kk_raw[:, b, :].unsqueeze(2).to_broadcast([P, PACK, 2]))
+            nc.scalar.copy(out=lin[b][:, :, 1:4:2], in_=km_raw[:, b, :].unsqueeze(2).to_broadcast([P, PACK, 2]))
+
+        def spread(column, tag):
+            ps = psum.tile([P, PACK, P], BF16, name="spread_ps", tag=tag)
+            for j in range(PACK):
+                nc.tensor.transpose(ps[:, j, :], column(j).to_broadcast([P, P]), ident_b[:])
+            return ps
+
+        for b in range(IMAGES):
+            tag = "vd" if b == 0 else "sd"
+            kk_ps = spread(lambda j: kk_raw[:, b, j : j + 1], tag)
+            nc.scalar.copy(out=kk_b[b][:], in_=kk_ps[:].rearrange("q j p -> q (j p)"))
+            km_ps = spread(lambda j: km_raw[:, b, j : j + 1], tag)
+            nc.scalar.copy(out=km_b[b][:], in_=km_ps[:].rearrange("q j p -> q (j p)"))
+            lp = psum.tile([P, PACK, P], BF16, name="lp", tag=tag)
+            for j in range(PACK):
+                nc.tensor.transpose(lp[:, j, :], lin[b][:, j, :], ident_b[:])
+            nc.scalar.copy(out=l_rows[b][:], in_=lp[:])
+        bo_ps = spread(lambda j: bo_raw[:, j : j + 1], "vd")
+        nc.scalar.copy(out=bo_b[:].rearrange("q (p j) -> q p j", j=PACK), in_=bo_ps[:].rearrange("q j p -> q p j"))
 
         m_ps = psum.tile([P, P], BF16, name="m_ps", tag="sd")
         nc.tensor.transpose(m_ps[:], m_raw[:], ident_b[:])
@@ -144,25 +157,6 @@ def tile_hydraattention_pb_t_kernel(tc, x, mask, W_q, b_q, kv_know, kv_mask, W_o
         nc.gpsimd.tensor_scalar(out=m07[:], in0=m_t[:], scalar1=0.7, scalar2=0.0, op0=ALU.mult, op1=ALU.add)
         nc.gpsimd.tensor_tensor(out=ab0[:, :, 0], in0=inv[:], in1=mix[:], op=ALU.mult)
         nc.gpsimd.tensor_tensor(out=ab0[:, :, 1], in0=m07[:], in1=m_t[:], op=ALU.mult)
-
-        def spread(label, tag):
-            ps = psum.tile([P, PACK, P], F32, name="spread_ps", tag=tag)
-            for j in range(PACK):
-                nc.tensor.transpose(ps[:, j, :], vec4[label][:, j : j + 1].to_broadcast([P, P]), ident_f[:])
-            return ps
-
-        for b in range(IMAGES):
-            tag = "vd" if b == 0 else "sd"
-            kk_ps = spread("kk%d" % b, tag)
-            nc.scalar.copy(out=kk_b[b][:], in_=kk_ps[:].rearrange("q j p -> q (j p)"))
-            km_ps = spread("km%d" % b, tag)
-            nc.scalar.copy(out=km_b[b][:], in_=km_ps[:].rearrange("q j p -> q (j p)"))
-            lp = psum.tile([P, PACK, P], BF16, name="lp", tag=tag)
-            for j in range(PACK):
-                nc.tensor.transpose(lp[:, j, :], lin[b][:, j, :], ident_b[:])
-            nc.scalar.copy(out=l_rows[b][:], in_=lp[:])
-        bo_ps = spread("bo", "vd")
-        nc.scalar.copy(out=bo_b[:].rearrange("q (p j) -> q p j", j=PACK), in_=bo_ps[:].rearrange("q j p -> q p j"))
 
         def quantise_w_out():
             wo_grp = work.tile([P, C, PACK], BF16, name="wo_grp", tag="gg", align_bytes=64)

@@ -80,13 +80,13 @@ def tile_hydraattention_pb_t_kernel(tc, x, mask, W_q, b_q, kv_know, kv_mask, W_o
         for b in range(IMAGES):
             xv = x[b].rearrange("(p j) h w -> p j (h w)", j=PACK)
             for k in range(NPIX // XLOAD):
-                xr = xpool.tile([P, PACK, XLOAD], BF16, name="x_raw%d_%d" % (b, k))
-                if b == 0 and k == 0:
-                    nc.sync.dma_start(out=xr[:, :, 0:CHUNK], in_=xv[:, :, 0:CHUNK])
-                    nc.sync.dma_start(out=xr[:, :, CHUNK:XLOAD], in_=xv[:, :, CHUNK:XLOAD])
-                else:
-                    nc.sync.dma_start(out=xr[:], in_=xv[:, :, k * XLOAD : (k + 1) * XLOAD])
-                x_raw.append(xr)
+                parts = 2 if b == 0 and k == 0 else 1
+                width = XLOAD // parts
+                for part in range(parts):
+                    xr = xpool.tile([P, PACK, width], BF16, name="x_raw%d_%d_%d" % (b, k, part))
+                    t0 = k * XLOAD + part * width
+                    nc.sync.dma_start(out=xr[:], in_=xv[:, :, t0 : t0 + width])
+                    x_raw.extend([xr[:, :, c : c + CHUNK] for c in range(0, width, CHUNK)])
                 if b == 0 and k == 1:
                     nc.sync.dma_start(out=wo_raw[:], in_=W_out.rearrange("(p j) o -> p j o", j=PACK))
 
@@ -113,13 +113,20 @@ def tile_hydraattention_pb_t_kernel(tc, x, mask, W_q, b_q, kv_know, kv_mask, W_o
             nc.vector.memset(lin[k][:], 0.0)
 
         wq_grp = const.tile([P, C, PACK], BF16, name="wq_grp", align_bytes=64)
-        nc.vector.tensor_copy(
-            out=wq_grp[:].rearrange("q (j p) k -> q j p k", j=PACK),
-            in_=wq_raw[:].rearrange("q k (p j) -> q j p k", j=PACK),
-        )
-        nc.vector.quantize_mx(
-            out=wq_codes[:].bitcast(FP8X4), scales=wq_sc[:], in_=wq_grp[:].rearrange("q c k -> q (c k)")
-        )
+        wq_out = wq_grp[:].rearrange("q (j p) k -> q j p k", j=PACK)
+        wq_in = wq_raw[:].rearrange("q k (p j) -> q j p k", j=PACK)
+        nc.vector.tensor_copy(out=wq_out[:, 0:2], in_=wq_in[:, 0:2])
+        nc.scalar.copy(out=wq_out[:, 2:4], in_=wq_in[:, 2:4])
+
+        def quantise_w_q(h):
+            half = slice(h * C // 2, (h + 1) * C // 2)
+            nc.vector.quantize_mx(
+                out=wq_codes[:, half].bitcast(FP8X4),
+                scales=wq_sc[:, half],
+                in_=wq_grp[:, half, :].rearrange("q c k -> q (c k)"),
+            )
+
+        quantise_w_q(0)
 
         nc.scalar.copy(out=bq4[:], in_=bq_raw[:])
         for b in range(IMAGES):
@@ -132,13 +139,13 @@ def tile_hydraattention_pb_t_kernel(tc, x, mask, W_q, b_q, kv_know, kv_mask, W_o
                 nc.tensor.transpose(ps[:, j, :], column(j).to_broadcast([P, P]), ident_b[:])
             return ps
 
+        tags = ("vd", "sd")
+        for raw, row in ((kk_raw, kk_b), (km_raw, km_b)):
+            for b in range(IMAGES):
+                ps = spread(lambda j: raw[:, b, j : j + 1], tags[b])
+                nc.scalar.copy(out=row[b][:], in_=ps[:].rearrange("q j p -> q (j p)"))
         for b in range(IMAGES):
-            tag = "vd" if b == 0 else "sd"
-            kk_ps = spread(lambda j: kk_raw[:, b, j : j + 1], tag)
-            nc.scalar.copy(out=kk_b[b][:], in_=kk_ps[:].rearrange("q j p -> q (j p)"))
-            km_ps = spread(lambda j: km_raw[:, b, j : j + 1], tag)
-            nc.scalar.copy(out=km_b[b][:], in_=km_ps[:].rearrange("q j p -> q (j p)"))
-            lp = psum.tile([P, PACK, P], BF16, name="lp", tag=tag)
+            lp = psum.tile([P, PACK, P], BF16, name="lp", tag=tags[b])
             for j in range(PACK):
                 nc.tensor.transpose(lp[:, j, :], lin[b][:, j, :], ident_b[:])
             nc.scalar.copy(out=l_rows[b][:], in_=lp[:])
@@ -176,18 +183,16 @@ def tile_hydraattention_pb_t_kernel(tc, x, mask, W_q, b_q, kv_know, kv_mask, W_o
             return 0 <= i < N_CHUNKS
 
         def regroup_x(i):
-            xr = x_raw[i // 2]
-            off = (i % 2) * CHUNK
             xg = xgp.tile([P, CHUNK, PACK], BF16, name="xg", tag="xg", align_bytes=64)
             if i < V_REGROUPS:
                 nc.vector.tensor_copy(
                     out=xg[:].rearrange("p (c i) j -> p c j i", i=PACK),
-                    in_=xr[:, :, off : off + CHUNK].rearrange("p j (c i) -> p c j i", i=PACK),
+                    in_=x_raw[i].rearrange("p j (c i) -> p c j i", i=PACK),
                 )
             else:
                 nc.gpsimd.tensor_scalar(
                     out=xg[:],
-                    in0=xr[:, :, off : off + CHUNK].rearrange("p j t -> p t j"),
+                    in0=x_raw[i].rearrange("p j t -> p t j"),
                     scalar1=1.0,
                     scalar2=0.0,
                     op0=ALU.mult,
@@ -409,6 +414,8 @@ def tile_hydraattention_pb_t_kernel(tc, x, mask, W_q, b_q, kv_know, kv_mask, W_o
                     quantise_g(s - 6)
                 if live(s - 1):
                     quantise_x(s - 1)
+                if s == 1:
+                    quantise_w_q(1)
                 if live(s):
                     regroup_x(s)
                 if live(s - 5):

from contextlib import ExitStack

import concourse.mybir as mybir
from concourse.masks import make_identity

F32 = mybir.dt.float32
BF16 = mybir.dt.bfloat16
U32 = mybir.dt.uint32
U8 = mybir.dt.uint8
FP8X4 = mybir.dt.float8_e4m3fn_x4
ACT = mybir.ActivationFunctionType
ALU = mybir.AluOpType

P = 128
PACK = 4
C = 512
NPIX = 4096
IMAGES = 2
CHUNK = 512
TILES = CHUNK // P
CHUNKS_PER_IMAGE = NPIX // CHUNK
N_CHUNKS = IMAGES * CHUNKS_PER_IMAGE
N_TILES = N_CHUNKS * TILES
XLOAD = 1024
WALK = 2
V_HELP_STEPS = 7
V_REGROUPS = 5
PE_FULL_CHUNKS = 3
S_BANK_FIRST = 11
S_BANK_LAST = 14


def pe_tiles(i):
    return TILES if i < PE_FULL_CHUNKS else TILES - 1


def scalar_empties_y(i, tt):
    return S_BANK_FIRST <= i <= S_BANK_LAST and tt == 0


def vector_empties_q(i, j):
    return i + 2 < V_HELP_STEPS and j % 2 == 1


FLOPS = 2 * 2 * IMAGES * NPIX * C * C


def tile_hydraattention_pb_t_kernel(tc, x, mask, W_q, b_q, kv_know, kv_mask, W_out, b_out, out):
    nc = tc.nc
    with ExitStack() as ctx:
        const = ctx.enter_context(tc.tile_pool(name="const", bufs=1))
        xpool = ctx.enter_context(tc.tile_pool(name="xpool", bufs=1))
        psum = ctx.enter_context(tc.psum_pool(name="psum", bufs=4))
        xq = ctx.enter_context(tc.tile_pool(name="xq", bufs=3))
        upool = ctx.enter_context(tc.tile_pool(name="upool", bufs=6))
        small = ctx.enter_context(tc.tile_pool(name="small", bufs=3))
        work = ctx.enter_context(tc.tile_pool(name="work", bufs=2))
        gq = ctx.enter_context(tc.tile_pool(name="gq", bufs=3))
        xgp = ctx.enter_context(tc.tile_pool(name="xgp", bufs=1))
        ypool = ctx.enter_context(tc.tile_pool(name="ypool", bufs=3))

        wq_codes = const.tile([P, C], U32, name="wq_codes", align_bytes=64)
        wq_sc = const.tile([P, C], U8, name="wq_sc", align_bytes=64)
        wo_codes = const.tile([P, C], U32, name="wo_codes", align_bytes=64)
        wo_sc = const.tile([P, C], U8, name="wo_sc", align_bytes=64)
        ident_f = const.tile([P, P], F32, name="ident_f")
        ident_b = const.tile([P, P], BF16, name="ident_b")
        bq4 = const.tile([P, PACK], F32, name="bq4")
        bo_b = const.tile([P, C], BF16, name="bo_b")
        ab0 = const.tile([P, N_TILES, 2], F32, name="ab0")
        l_rows = [const.tile([P, PACK, P], BF16, name="l_rows%d" % b) for b in range(IMAGES)]
        kk_b = [const.tile([P, C], BF16, name="kk_b%d" % b) for b in range(IMAGES)]
        km_b = [const.tile([P, C], BF16, name="km_b%d" % b) for b in range(IMAGES)]
        r_in = [const.tile([P, TILES, P], BF16, name="r_in%d" % k) for k in range(2)]

        wq_raw = work.tile([P, PACK, C], BF16, name="wq_raw", tag="gg", align_bytes=64)
        nc.sync.dma_start(out=wq_raw[:], in_=W_q.rearrange("(p j) c -> p j c", j=PACK))
        wo_raw = work.tile([P, PACK, C], BF16, name="wo_raw", tag="gg", align_bytes=64)
        x_raw = []
        for b in range(IMAGES):
            xv = x[b].rearrange("(p j) h w -> p j (h w)", j=PACK)
            for k in range(NPIX // XLOAD):
                parts = 2 if b == 0 and k == 0 else 1
                width = XLOAD // parts
                for part in range(parts):
                    xr = xpool.tile([P, PACK, width], BF16, name="x_raw%d_%d_%d" % (b, k, part))
                    t0 = k * XLOAD + part * width
                    nc.sync.dma_start(out=xr[:], in_=xv[:, :, t0 : t0 + width])
                    x_raw.extend([xr[:, :, c : c + CHUNK] for c in range(0, width, CHUNK)])
                if b == 0 and k == 1:
                    nc.sync.dma_start(out=wo_raw[:], in_=W_out.rearrange("(p j) o -> p j o", j=PACK))

        bq_raw = const.tile([P, PACK], BF16, name="bq_raw")
        nc.scalar.dma_start(out=bq_raw[:], in_=b_q.rearrange("(p j) -> p j", j=PACK))
        kk_raw = const.tile([P, IMAGES, PACK], BF16, name="kk_raw")
        nc.scalar.dma_start(out=kk_raw[:], in_=kv_know.rearrange("b o (p j) -> p (b o) j", j=PACK))
        km_raw = const.tile([P, IMAGES, PACK], BF16, name="km_raw")
        nc.scalar.dma_start(out=km_raw[:], in_=kv_mask.rearrange("b o (p j) -> p (b o) j", j=PACK))
        bo_raw = const.tile([P, PACK], BF16, name="bo_raw")
        nc.scalar.dma_start(out=bo_raw[:], in_=b_out.rearrange("(p j) -> p j", j=PACK))
        m_raw = const.tile([P, P], BF16, name="m_raw")
        nc.vector.memset(m_raw[:], 0.0)
        nc.scalar.dma_start(out=m_raw[0:N_TILES, :], in_=mask.rearrange("b o (g h) w -> (b o g) (h w)", h=2))

        warm = const.tile([P, 1], F32, name="warm")
        nc.vector.memset(warm[:], 1.0)
        nc.scalar.activation(out=warm[:], in_=warm[:], func=ACT.Abs_reciprocal_sqrt)
        make_identity(nc, ident_b[:])
        make_identity(nc, ident_f[:])
        lin = [const.tile([P, PACK, P], BF16, name="lin%d" % b) for b in range(IMAGES)]
        for k in range(2):
            nc.vector.memset(r_in[k][:], 0.0)
            nc.vector.memset(lin[k][:], 0.0)

        wq_grp = const.tile([P, C, PACK], BF16, name="wq_grp", align_bytes=64)
        wq_out = wq_grp[:].rearrange("q (j p) k -> q j p k", j=PACK)
        wq_in = wq_raw[:].rearrange("q k (p j) -> q j p k", j=PACK)
        nc.vector.tensor_copy(out=wq_out[:, 0:2], in_=wq_in[:, 0:2])
        nc.scalar.copy(out=wq_out[:, 2:4], in_=wq_in[:, 2:4])

        def quantise_w_q(h):
            half = slice(h * C // 2, (h + 1) * C // 2)
            nc.vector.quantize_mx(
                out=wq_codes[:, half].bitcast(FP8X4),
                scales=wq_sc[:, half],
                in_=wq_grp[:, half, :].rearrange("q c k -> q (c k)"),
            )

        quantise_w_q(0)

        nc.scalar.copy(out=bq4[:], in_=bq_raw[:])
        for b in range(IMAGES):
            nc.scalar.copy(out=lin[b][:, :, 0:4:2], in_=kk_raw[:, b, :].unsqueeze(2).to_broadcast([P, PACK, 2]))
            nc.scalar.copy(out=lin[b][:, :, 1:4:2], in_=km_raw[:, b, :].unsqueeze(2).to_broadcast([P, PACK, 2]))

        def spread(column, tag):
            ps = psum.tile([P, PACK, P], BF16, name="spread_ps", tag=tag)
            for j in range(PACK):
                nc.tensor.transpose(ps[:, j, :], column(j).to_broadcast([P, P]), ident_b[:])
            return ps

        tags = ("vd", "sd")
        for raw, row in ((kk_raw, kk_b), (km_raw, km_b)):
            for b in range(IMAGES):
                ps = spread(lambda j: raw[:, b, j : j + 1], tags[b])
                nc.scalar.copy(out=row[b][:], in_=ps[:].rearrange("q j p -> q (j p)"))
        for b in range(IMAGES):
            lp = psum.tile([P, PACK, P], BF16, name="lp", tag=tags[b])
            for j in range(PACK):
                nc.tensor.transpose(lp[:, j, :], lin[b][:, j, :], ident_b[:])
            nc.scalar.copy(out=l_rows[b][:], in_=lp[:])
        bo_ps = spread(lambda j: bo_raw[:, j : j + 1], "vd")
        nc.scalar.copy(out=bo_b[:].rearrange("q (p j) -> q p j", j=PACK), in_=bo_ps[:].rearrange("q j p -> q p j"))

        m_ps = psum.tile([P, P], BF16, name="m_ps", tag="sd")
        nc.tensor.transpose(m_ps[:], m_raw[:], ident_b[:])
        m_t = const.tile([P, N_TILES], F32, name="m_t")
        nc.scalar.copy(out=m_t[:], in_=m_ps[:, 0:N_TILES])
        inv = const.tile([P, N_TILES], F32, name="inv")
        nc.gpsimd.tensor_scalar(out=inv[:], in0=m_t[:], scalar1=-1.0, scalar2=1.0, op0=ALU.mult, op1=ALU.add)
        mix = const.tile([P, N_TILES], F32, name="mix")
        nc.gpsimd.tensor_scalar(out=mix[:], in0=m_t[:], scalar1=-0.7, scalar2=1.0, op0=ALU.mult, op1=ALU.add)
        m07 = const.tile([P, N_TILES], F32, name="m07")
        nc.gpsimd.tensor_scalar(out=m07[:], in0=m_t[:], scalar1=0.7, scalar2=0.0, op0=ALU.mult, op1=ALU.add)
        nc.gpsimd.tensor_tensor(out=ab0[:, :, 0], in0=inv[:], in1=mix[:], op=ALU.mult)
        nc.gpsimd.tensor_tensor(out=ab0[:, :, 1], in0=m07[:], in1=m_t[:], op=ALU.mult)

        def quantise_w_out():
            wo_grp = work.tile([P, C, PACK], BF16, name="wo_grp", tag="gg", align_bytes=64)
            nc.scalar.copy(
                out=wo_grp[:].rearrange("p (c i) j -> p c j i", i=PACK), in_=wo_raw[:].rearrange("p j (c i) -> p c j i", i=PACK)
            )
            state["wo_grp"] = wo_grp

        def quantise_w_out2():
            nc.vector.quantize_mx(
                out=wo_codes[:].bitcast(FP8X4), scales=wo_sc[:], in_=state["wo_grp"][:].rearrange("p o j -> p (o j)")
            )

        state = {}

        def live(i):
            return 0 <= i < N_CHUNKS

        def regroup_x(i):
            xg = xgp.tile([P, CHUNK, PACK], BF16, name="xg", tag="xg", align_bytes=64)
            if i < V_REGROUPS:
                nc.vector.tensor_copy(
                    out=xg[:].rearrange("p (c i) j -> p c j i", i=PACK),
                    in_=x_raw[i].rearrange("p j (c i) -> p c j i", i=PACK),
                )
            else:
                nc.gpsimd.tensor_scalar(
                    out=xg[:],
                    in0=x_raw[i].rearrange("p j t -> p t j"),
                    scalar1=1.0,
                    scalar2=0.0,
                    op0=ALU.mult,
                    op1=ALU.add,
                )
            state[("xg", i)] = xg

        def quantise_x(i):
            xg = state[("xg", i)]
            xc = xq.tile([P, CHUNK], U32, name="xc", align_bytes=64)
            xs = xq.tile([P, CHUNK], U8, name="xs", align_bytes=64)
            nc.vector.quantize_mx(out=xc[:].bitcast(FP8X4), scales=xs[:], in_=xg[:].rearrange("p t j -> p (t j)"))
            state[("x", i)] = (xc, xs)

        def project_q(i, j):
            xc, xs = state[("x", i)]
            q = psum.tile([P, CHUNK], F32, name="q", tag="vd" if vector_empties_q(i, j) else "sd")
            nc.tensor.matmul_mx(
                out=q[:],
                lhsT=wq_codes[:, j * P : (j + 1) * P].bitcast(FP8X4),
                lhsT_scale=wq_sc[:, j * P : (j + 1) * P],
                rhs=xc[:].bitcast(FP8X4),
                rhs_scale=xs[:],
                start=True,
                stop=True,
            )
            state[("q", i, j)] = q

        def empty_q(i, j):
            if j == 0:
                state[("u", i)] = upool.tile([P, PACK, CHUNK], F32, name="u")
            u = state[("u", i)]
            q = state[("q", i, j)]
            if vector_empties_q(i, j):
                nc.vector.tensor_scalar(out=u[:, j, :], in0=q[:], scalar1=bq4[:, j : j + 1], scalar2=None, op0=ALU.add)
            else:
                nc.scalar.activation(out=u[:, j, :], in_=q[:], func=ACT.Identity, bias=bq4[:, j : j + 1], scale=1.0)

        def pixel_rows(i, tt):
            u = state[("u", i)]
            ut = psum.tile([P, C], F32, name="ut", tag="sd")
            for j in range(PACK):
                nc.tensor.transpose(ut[:, j * P : (j + 1) * P], u[:, j, tt * P : (tt + 1) * P], ident_f[:])
            state[("ut", i, tt)] = ut

        def square_sum(i, tt):
            if tt == 0:
                state[("n2", i)] = small.tile([P, TILES], F32, name="n2")
            n2 = state[("n2", i)]
            ut = state[("ut", i, tt)]
            junk = work.tile([P, C], BF16, name="junk")
            nc.scalar.activation(out=junk[:], in_=ut[:], func=ACT.Square, accum_out=n2[:, tt : tt + 1])

        def norm(i):
            rn = small.tile([P, TILES], F32, name="rn")
            nc.scalar.activation(out=rn[:], in_=state[("n2", i)][:], func=ACT.Abs_reciprocal_sqrt)
            state[("rn", i)] = rn

        def factor_chain(i):
            rn = state[("rn", i)]
            ab = small.tile([P, TILES, 2], F32, name="ab")
            rin = r_in[i % 2]
            state[("ab", i)] = ab
            nc.gpsimd.tensor_tensor(
                out=ab[:],
                in0=ab0[:, i * TILES : (i + 1) * TILES, :],
                in1=rn[:].unsqueeze(2).to_broadcast([P, TILES, 2]),
                op=ALU.mult,
            )
            nc.gpsimd.tensor_tensor(
                out=rin[:, 0 : pe_tiles(i), 0:2],
                in0=ab0[:, i * TILES : i * TILES + pe_tiles(i), :],
                in1=rn[:, 0 : pe_tiles(i)].unsqueeze(2).to_broadcast([P, pe_tiles(i), 2]),
                op=ALU.mult,
            )
            nc.gpsimd.tensor_tensor(out=rin[:, 0 : pe_tiles(i), 2:4], in0=ab[:, 0 : pe_tiles(i), :], in1=rin[:, 0 : pe_tiles(i), 0:2], op=ALU.subtract)

        def scale_row(out_t, in_t, factor, on_g):
            if on_g:
                nc.gpsimd.tensor_scalar(out=out_t[:], in0=in_t[:], scalar1=factor, scalar2=0.0, op0=ALU.mult, op1=ALU.add)
            else:
                nc.scalar.activation(out=out_t[:], in_=in_t[:], func=ACT.Copy, scale=factor)

        def gate_last_tile(i):
            if pe_tiles(i) == TILES:
                return
            b = i // CHUNKS_PER_IMAGE
            ab = state[("ab", i)]
            zk = work.tile([P, C], F32, name="zk")
            scale_row(zk, kk_b[b], ab[:, pe_tiles(i), 0:1], False)
            zm = work.tile([P, C], F32, name="zm")
            scale_row(zm, km_b[b], ab[:, pe_tiles(i), 1:2], True)
            state[("wt", i)] = (zk, zm)

        def factor_rows(i):
            rin = r_in[i % 2]
            rp = psum.tile([P, TILES, P], BF16, name="rp", tag="sd")
            for tt in range(pe_tiles(i)):
                nc.tensor.transpose(rp[:, tt, :], rin[:, tt, :], ident_b[:])
            rows = work.tile([P, TILES, P], BF16, name="rows")
            nc.scalar.copy(out=rows[:, 0 : pe_tiles(i), :], in_=rp[:, 0 : pe_tiles(i), :])
            state[("rows", i)] = rows

        def gate_factor(i, tt):
            b = i // CHUNKS_PER_IMAGE
            wb = psum.tile([P, PACK, P], F32, name="wb", tag="vd")
            if tt < pe_tiles(i):
                rows = state[("rows", i)]
                for j in range(PACK):
                    nc.tensor.matmul(out=wb[:, j, :], lhsT=l_rows[b][:, j, :], rhs=rows[:, tt, :], start=True, stop=True)
            else:
                zk, zm = state[("wt", i)]
                for j in range(PACK):
                    cols = slice(j * P, (j + 1) * P)
                    nc.tensor.matmul(
                        out=wb[:, j, :], lhsT=zk[:, cols], rhs=ident_f[:], is_transpose=True, start=True, stop=False
                    )
                    nc.tensor.matmul(
                        out=wb[:, j, :], lhsT=zm[:, cols], rhs=ident_f[:], is_transpose=True, start=False, stop=True
                    )
            state[("wb", i, tt)] = wb

        def gate(i, tt):
            u = state[("u", i)]
            if tt == 0:
                state[("gg", i)] = work.tile([P, CHUNK, PACK], BF16, name="gg", align_bytes=64)
            gg = state[("gg", i)]
            wb = state[("wb", i, tt)]
            nc.vector.tensor_tensor(
                out=gg[:, tt * P : (tt + 1) * P, :].rearrange("p (c i) j -> p c j i", i=WALK),
                in0=u[:, :, tt * P : (tt + 1) * P].rearrange("p j (c i) -> p c j i", i=WALK),
                in1=wb[:].rearrange("p j (c i) -> p c j i", i=WALK),
                op=ALU.mult,
            )

        def quantise_g(i):
            gg = state[("gg", i)]
            gc = gq.tile([P, CHUNK], U32, name="gc", align_bytes=64)
            gs = gq.tile([P, CHUNK], U8, name="gs", align_bytes=64)
            nc.vector.quantize_mx(out=gc[:].bitcast(FP8X4), scales=gs[:], in_=gg[:].rearrange("p t j -> p (t j)"))
            state[("g", i)] = (gc, gs)

        def project_out(i, tt):
            gc, gs = state[("g", i)]
            y = psum.tile([P, C], F32, name="y", tag="sd" if scalar_empties_y(i, tt) else "vd")
            nc.tensor.matmul_mx(
                out=y[:],
                lhsT=gc[:, tt * P : (tt + 1) * P].bitcast(FP8X4),
                lhsT_scale=gs[:, tt * P : (tt + 1) * P],
                rhs=wo_codes[:].bitcast(FP8X4),
                rhs_scale=wo_sc[:],
                start=True,
                stop=True,
            )
            state[("y", i, tt)] = y

        def empty_y(i, tt):
            if tt == 0:
                state[("yo", i)] = ypool.tile([P, TILES, C], F32, name="yo")
            yo = state[("yo", i)]
            y = state[("y", i, tt)]
            if scalar_empties_y(i, tt):
                nc.scalar.copy(out=yo[:, tt, :], in_=y[:])
            else:
                nc.vector.tensor_tensor(out=yo[:, tt, :], in0=y[:], in1=bo_b[:], op=ALU.add)
                store_tile(i, tt)

        def add_y(i, tt):
            yo = state[("yo", i)]
            if scalar_empties_y(i, tt):
                nc.gpsimd.tensor_tensor(out=yo[:, tt, :], in0=yo[:, tt, :], in1=bo_b[:], op=ALU.add)
                store_tile(i, tt)

        def store_tile(i, tt):
            yo = state[("yo", i)]
            if i == N_CHUNKS - 1:
                b = i // CHUNKS_PER_IMAGE
                t0 = (i % CHUNKS_PER_IMAGE) * CHUNK + tt * P
                nc.sync.dma_start(out=out[b, t0 : t0 + P, :], in_=yo[:, tt, :])

        def store(i):
            if i == N_CHUNKS - 1:
                return
            b = i // CHUNKS_PER_IMAGE
            t0 = (i % CHUNKS_PER_IMAGE) * CHUNK
            nc.sync.dma_start(
                out=out[b, t0 : t0 + CHUNK, :].rearrange("(tt p) o -> p tt o", p=P), in_=state[("yo", i)][:]
            )

        with tc.manual_schedule():
            for s in range(N_CHUNKS + 8):
                if live(s - 2):
                    project_q(s - 2, 0)
                    empty_q(s - 2, 0)
                if live(s - 7):
                    project_out(s - 7, 0)
                    empty_y(s - 7, 0)
                if live(s - 2):
                    project_q(s - 2, 1)
                    empty_q(s - 2, 1)
                if live(s - 7):
                    project_out(s - 7, 1)
                    empty_y(s - 7, 1)
                if live(s - 4):
                    factor_chain(s - 4)
                if live(s - 2):
                    project_q(s - 2, 2)
                    empty_q(s - 2, 2)
                if live(s - 7):
                    project_out(s - 7, 2)
                    empty_y(s - 7, 2)
                if live(s - 2):
                    project_q(s - 2, 3)
                    empty_q(s - 2, 3)
                if live(s - 7):
                    project_out(s - 7, 3)
                    empty_y(s - 7, 3)
                if live(s - 6):
                    quantise_g(s - 6)
                if live(s - 1):
                    quantise_x(s - 1)
                if s == 1:
                    quantise_w_q(1)
                if live(s):
                    regroup_x(s)
                if live(s - 5):
                    gate_factor(s - 5, 0)
                    gate(s - 5, 0)
                    gate_factor(s - 5, 1)
                    gate(s - 5, 1)
                    gate_factor(s - 5, 2)
                    gate(s - 5, 2)
                if live(s - 3):
                    pixel_rows(s - 3, 0)
                    square_sum(s - 3, 0)
                    pixel_rows(s - 3, 1)
                    square_sum(s - 3, 1)
                    pixel_rows(s - 3, 2)
                    square_sum(s - 3, 2)
                    pixel_rows(s - 3, 3)
                    square_sum(s - 3, 3)
                if live(s - 5):
                    gate_factor(s - 5, 3)
                    gate(s - 5, 3)
                if live(s - 4):
                    factor_rows(s - 4)
                if live(s - 3):
                    norm(s - 3)
                if live(s - 4):
                    gate_last_tile(s - 4)
                if live(s - 7):
                    add_y(s - 7, 0)
                    add_y(s - 7, 1)
                    add_y(s - 7, 2)
                    add_y(s - 7, 3)
                    store(s - 7)
                if s == 2:
                    quantise_w_out()
                if s == 3:
                    quantise_w_out2()
